import numpy as np
import ml_dtypes


def mxq(x, axis, fmt="e4m3"):
    dtype, down = {"e4m3": (ml_dtypes.float8_e4m3fn, 7), "e5m2": (ml_dtypes.float8_e5m2, 14)}[fmt]
    v = np.moveaxis(np.asarray(x, np.float32).astype(ml_dtypes.bfloat16).astype(np.float64), axis, -1)
    blocks = v.reshape(v.shape[:-1] + (-1, 32))
    amax = np.abs(blocks).max(-1, keepdims=True)
    byte = np.maximum(np.where(amax > 0, np.frexp(amax)[1] - 1 + 127, 0) - down, 1)
    scale = np.exp2(byte - 127.0)
    codes = (blocks / scale).astype(np.float32).astype(dtype).astype(np.float64)
    return np.moveaxis((codes * scale).reshape(v.shape), -1, axis)


WIDE = False


def mx_kscale(k):
    if not WIDE:
        return np.ones(k)
    levels = np.array([10, -10, 5, -5, 0])
    a = np.random.permutation(np.resize(levels, k // 512 * 4)).reshape(k // 512, 4)
    idx = np.arange(k)
    return np.exp2(a[idx // 512, idx % 128 // 32])


BF16 = ml_dtypes.bfloat16


def bf(x):
    return np.asarray(x, np.float32).astype(BF16)


def f64(x):
    return np.asarray(x).astype(np.float64)


B, N, CIN, COUT = 4, 512, 512, 256


def xavier():
    return np.random.uniform(-1.0, 1.0, (CIN, COUT)) * (1.414 * np.sqrt(6.0 / (CIN + COUT)))


def setup_inputs():
    s = mx_kscale(CIN)
    return {"x": bf(np.random.standard_normal((B, N, CIN)) * s),
            "W": bf(np.stack([xavier(), xavier()]) / s[None, :, None]),
            "M": bf(1.0 + 0.1 * np.random.standard_normal((N, COUT))),
            "adj": bf(np.random.uniform(0.0, 1.0, (N, N)) * 1.5 / np.sqrt(N) + np.eye(N) * np.random.uniform(0.5, 1.5, (N, 1))),
            "adj2": bf(np.random.standard_normal((N, N)) * 0.5 / np.sqrt(N)),
            "bias": bf(np.random.standard_normal(COUT) * 0.5)}


def reference(x, W, M, adj, adj2, bias):
    xq = mxq(f64(x), 2, "e4m3")
    Wf = f64(W)
    h0 = xq @ mxq(Wf[0], 0, "e4m3")
    h1 = xq @ mxq(Wf[1], 0, "e4m3")
    A = f64(adj) + f64(adj2)
    A = (A.T + A) * 0.5
    E = np.eye(N)
    a_self = np.diagonal(A)
    a_off = A * (1.0 - E)
    g0 = f64(M) * h0
    g1 = f64(M) * h1
    agg = mxq(a_off, 1, "e4m3") @ mxq(g1, 1, "e4m3")
    return a_self[None, :, None] * g0 + agg + f64(bias)

@@ -1,0 +1,210 @@
+from contextlib import ExitStack
+
+import concourse.mybir as mybir
+from concourse.masks import make_identity
+
+FLOPS = 2 * 2048 * 512 * 512 + 4 * 2 * 512 * 512 * 256
+
+F32 = mybir.dt.float32
+BF16 = mybir.dt.bfloat16
+U32 = mybir.dt.uint32
+U8 = mybir.dt.uint8
+FP8X4 = mybir.dt.float8_e4m3fn_x4
+ALU = mybir.AluOpType
+ACT = mybir.ActivationFunctionType
+
+P = 128
+B = 4
+NODES = 512
+CIN = 512
+COUT = 256
+T = 4
+
+
+def tile_modulatedgraphconv_pa_kernel(tc, x, W, M, adj, adj2, bias, out):
+    nc = tc.nc
+    with ExitStack() as ctx:
+        const = ctx.enter_context(tc.tile_pool(name="const", bufs=1))
+        keep = ctx.enter_context(tc.tile_pool(name="keep", bufs=1))
+        psum = ctx.enter_context(tc.psum_pool(name="psum", bufs=2))
+
+        ident_f = const.tile([P, P], F32, name="ident_f")
+        make_identity(nc, ident_f[:])
+        warm_in = const.tile([P, 1], F32, name="warm_in")
+        nc.gpsimd.memset(warm_in[:], 0.0)
+        warm_out = const.tile([P, 1], F32, name="warm_out")
+        nc.scalar.activation(out=warm_out[:], in_=warm_in[:], func=ACT.Copy)
+        ident_b = const.tile([P, P], BF16, name="ident_b")
+        make_identity(nc, ident_b[:])
+        ones_b = const.tile([P, P], BF16, name="ones_b")
+        nc.gpsimd.memset(ones_b[:], 1.0)
+        brow = const.tile([P, COUT], BF16, name="brow")
+        nc.gpsimd.memset(brow[:], 0.0)
+        offmask = const.tile([P, P], F32, name="offmask")
+        nc.gpsimd.tensor_scalar(out=offmask[:], in0=ident_f[:], scalar1=-1.0, scalar2=1.0,
+                                op0=ALU.mult, op1=ALU.add)
+
+        w_raw = keep.tile([P, 4, 512], BF16, name="w_raw")
+        x_sb = [keep.tile([P, T * CIN], BF16, name="x_sb%d" % b) for b in range(B)]
+        m_sb = keep.tile([P, T, COUT], BF16, name="m_sb")
+        adj_sb = keep.tile([P, T, NODES], BF16, name="adj_sb")
+        adj2_sb = keep.tile([P, T, NODES], BF16, name="adj2_sb")
+        diag1 = keep.tile([P, T], BF16, name="diag1")
+        diag2 = keep.tile([P, T], BF16, name="diag2")
+
+        def load_x(b):
+            nc.sync.dma_start(out=x_sb[b][:], in_=x[b].rearrange("(p t) k -> p (t k)", t=T))
+
+        nc.sync.dma_start(out=w_raw[:], in_=W.rearrange("w (u q e) c -> q (w u) (e c)", u=2, q=P, e=2))
+        load_x(0)
+        nc.sync.dma_start(out=m_sb[:], in_=M.rearrange("(p t) c -> p t c", t=T))
+        load_x(1)
+        nc.sync.dma_start(out=adj_sb[:], in_=adj.rearrange("(p t) i -> p t i", t=T))
+        nc.sync.dma_start(out=adj2_sb[:], in_=adj2.rearrange("(p t) i -> p t i", t=T))
+        load_x(2)
+        load_x(3)
+
+        nc.scalar.dma_start(out=brow[0:1, :], in_=bias.rearrange("(o c) -> o c", o=1))
+        with nc.allow_non_contiguous_dma(reason="the 512 diagonal elements, one piece each"):
+            nc.scalar.dma_start(
+                out=diag1[:],
+                in_=adj.rearrange("a b -> (a b)")[0:NODES * NODES:NODES + 1].rearrange("(p t) -> p t", t=T))
+            nc.scalar.dma_start(
+                out=diag2[:],
+                in_=adj2.rearrange("a b -> (a b)")[0:NODES * NODES:NODES + 1].rearrange("(p t) -> p t", t=T))
+
+        w_g = keep.tile([P, 2, 4 * COUT], BF16, name="w_g", align_bytes=64)
+        w_c = keep.tile([P, 2 * COUT], U32, name="w_c", align_bytes=64)
+        w_s = keep.tile([P, 2 * COUT], U8, name="w_s", align_bytes=64)
+        for w in (1, 0):
+            nc.vector.tensor_copy(
+                out=w_g[:, w, :].rearrange("p (c i s) -> p c s i", i=4, s=4),
+                in_=w_raw[:, 2 * w:2 * w + 2, :].rearrange("p u (e c i) -> p c (u e) i", e=2, i=4))
+        for w in (1, 0):
+            cols = slice(w * COUT, (w + 1) * COUT)
+            nc.vector.quantize_mx(out=w_c[:, cols].bitcast(FP8X4), scales=w_s[:, cols], in_=w_g[:, w, :])
+
+        bias_ps = psum.tile([P, COUT], F32, tag="agg", name="bias_ps")
+        nc.tensor.matmul(out=bias_ps[:], lhsT=ones_b[:], rhs=brow[:], start=True, stop=True)
+        bias2 = keep.tile([P, 2, COUT], F32, name="bias2")
+        for r in range(2):
+            nc.scalar.copy(out=bias2[:, r, :], in_=bias_ps[:])
+        a_self = keep.tile([P, T], F32, name="a_self")
+        nc.gpsimd.tensor_tensor(out=a_self[:], in0=diag1[:], in1=diag2[:], op=ALU.add)
+        a_m = keep.tile([P, T, COUT], F32, name="a_m")
+
+        def make_a_m():
+            for t in range(T):
+                nc.scalar.activation(out=a_m[:, t, :], in_=m_sb[:, t, :], func=ACT.Copy,
+                                     scale=a_self[:, t:t + 1])
+
+        x_g = [keep.tile([P, T * P * 4], BF16, name="x_g%d" % b, align_bytes=64) for b in range(B)]
+        x_c = [keep.tile([P, T * P], U32, name="x_c%d" % b, align_bytes=64) for b in range(B)]
+        x_s = [keep.tile([P, T * P], U8, name="x_s%d" % b, align_bytes=64) for b in range(B)]
+        g_g = [keep.tile([P, COUT * 4], BF16, name="g_g%d" % b, align_bytes=64) for b in range(B)]
+        g_c = [keep.tile([P, COUT], U32, name="g_c%d" % b, align_bytes=64) for b in range(B)]
+        g_s = [keep.tile([P, COUT], U8, name="g_s%d" % b, align_bytes=64) for b in range(B)]
+        g0 = [keep.tile([P, T, COUT], F32, name="g0_%d" % b) for b in range(B)]
+        o_sb = [keep.tile([P, T, COUT], F32, name="o_sb%d" % b) for b in range(B)]
+
+        def transpose_x(b):
+            xw = x_sb[b][:].bitcast(F32)
+            gw = x_g[b][:].bitcast(F32).rearrange("p (t n u) -> p t n u", t=T, u=2)
+            for h in range(2):
+                xt = psum.tile([P, 2, 2, P], F32, tag="xt", name="xt_%d_%d" % (b, h))
+                for tt in range(2):
+                    for u in range(2):
+                        c0 = (2 * h + tt) * 256 + u * P
+                        nc.tensor.transpose(xt[:, tt, u, :], xw[:, c0:c0 + P], ident_f[:])
+                nc.scalar.copy(out=gw[:, 2 * h:2 * h + 2, :, :], in_=xt[:].rearrange("p t u n -> p t n u"))
+
+        def quantise_x(b):
+            nc.vector.quantize_mx(out=x_c[b][:].bitcast(FP8X4), scales=x_s[b][:], in_=x_g[b][:])
+
+        def stage1(b):
+            gv = g_g[b][:].rearrange("p (c t) -> p c t", t=T)
+            for ch in range(2):
+                h1 = psum.tile([P, T, P], F32, tag="h1", name="h1_%d_%d" % (b, ch))
+                wc = slice(COUT + ch * P, COUT + (ch + 1) * P)
+                for t in range(T):
+                    nodes = slice(t * P, (t + 1) * P)
+                    nc.tensor.matmul_mx(out=h1[:, t, :],
+                                        lhsT=x_c[b][:, nodes].bitcast(FP8X4), lhsT_scale=x_s[b][:, nodes],
+                                        rhs=w_c[:, wc].bitcast(FP8X4), rhs_scale=w_s[:, wc],
+                                        start=True, stop=True)
+                cc = slice(ch * P, (ch + 1) * P)
+                nc.vector.tensor_tensor(out=gv[:, cc, :], in0=h1[:].rearrange("p t c -> p c t"),
+                                        in1=m_sb[:, :, cc].rearrange("p t c -> p c t"), op=ALU.mult)
+            nc.vector.quantize_mx(out=g_c[b][:].bitcast(FP8X4), scales=g_s[b][:], in_=g_g[b][:])
+            for h in range(2):
+                h0 = psum.tile([P, 2, COUT], F32, tag="h0", name="h0_%d_%d" % (b, h))
+                for tt in range(2):
+                    nodes = slice((2 * h + tt) * P, (2 * h + tt + 1) * P)
+                    nc.tensor.matmul_mx(out=h0[:, tt, :],
+                                        lhsT=x_c[b][:, nodes].bitcast(FP8X4), lhsT_scale=x_s[b][:, nodes],
+                                        rhs=w_c[:, 0:COUT].bitcast(FP8X4), rhs_scale=w_s[:, 0:COUT],
+                                        start=True, stop=True)
+                ts = slice(2 * h, 2 * h + 2)
+                nc.vector.tensor_tensor(out=g0[b][:, ts, :], in0=h0[:], in1=a_m[:, ts, :], op=ALU.mult)
+                nc.gpsimd.tensor_tensor(out=g0[b][:, ts, :], in0=g0[b][:, ts, :], in1=bias2[:], op=ALU.add)
+
+        s_perm = keep.tile([P, T, NODES], F32, name="s_perm")
+        a_g = keep.tile([P, NODES * 4], BF16, name="a_g", align_bytes=64)
+        a_c = keep.tile([P, NODES], U32, name="a_c", align_bytes=64)
+        a_s = keep.tile([P, NODES], U8, name="a_s", align_bytes=64)
+
+        def a_sum_rows():
+            for t in range(T):
+                s_ps = psum.tile([P, NODES], F32, tag="agg", name="s_ps%d" % t)
+                nc.tensor.matmul(out=s_ps[:], lhsT=ident_b[:], rhs=adj_sb[:, t, :], start=True, stop=False)
+                nc.tensor.matmul(out=s_ps[:], lhsT=ident_b[:], rhs=adj2_sb[:, t, :], start=False, stop=True)
+                nc.scalar.activation(out=s_perm[:, t, :].rearrange("p (s c) -> p s c", s=T),
+                                     in_=s_ps[:].rearrange("p (c s) -> p s c", s=T),
+                                     func=ACT.Copy, scale=0.5)
+                blk = s_perm[:, t, t * P:(t + 1) * P]
+                nc.gpsimd.tensor_tensor(out=blk, in0=blk, in1=offmask[:], op=ALU.mult)
+
+        def a_symmetrise():
+            av = a_g[:].rearrange("p (c t) -> p c t", t=T)
+            for tp in range(T):
+                tr = psum.tile([P, T, P], F32, tag="agg", name="tr%d" % tp)
+                for t in range(T):
+                    nc.tensor.transpose(tr[:, t, :], s_perm[:, tp, t * P:(t + 1) * P], ident_f[:])
+                cc = slice(tp * P, (tp + 1) * P)
+                nc.vector.tensor_tensor(out=av[:, cc, :], in0=tr[:].rearrange("p t c -> p c t"),
+                                        in1=s_perm[:, :, cc].rearrange("p t c -> p c t"), op=ALU.add)
+            nc.vector.quantize_mx(out=a_c[:].bitcast(FP8X4), scales=a_s[:], in_=a_g[:])
+
+        def stage2(b):
+            ov = out[b].rearrange("(p t) c -> p t c", t=T)
+            for h in range(2):
+                agg = psum.tile([P, 2, COUT], F32, tag="agg", name="agg_%d_%d" % (b, h))
+                for tt in range(2):
+                    rows = slice((2 * h + tt) * P, (2 * h + tt + 1) * P)
+                    nc.tensor.matmul_mx(out=agg[:, tt, :],
+                                        lhsT=a_c[:, rows].bitcast(FP8X4), lhsT_scale=a_s[:, rows],
+                                        rhs=g_c[b][:].bitcast(FP8X4), rhs_scale=g_s[b][:],
+                                        start=True, stop=True)
+                ts = slice(2 * h, 2 * h + 2)
+                nc.vector.tensor_tensor(out=o_sb[b][:, ts, :], in0=agg[:], in1=g0[b][:, ts, :], op=ALU.add)
+                nc.sync.dma_start(out=ov[:, ts, :], in_=o_sb[b][:, ts, :])
+
+        transpose_x(0)
+        make_a_m()
+        quantise_x(0)
+        transpose_x(1)
+        stage1(0)
+        quantise_x(1)
+        a_sum_rows()
+        stage1(1)
+        transpose_x(2)
+        a_symmetrise()
+        quantise_x(2)
+        stage2(0)
+        stage1(2)
+        transpose_x(3)
+        stage2(1)
+        quantise_x(3)
+        stage1(3)
+        stage2(2)
+        stage2(3)

@@ -20,6 +20,20 @@ CIN = 512
 COUT = 256
 T = 4
 
+MANUAL = True
+ORDER = (
+    "XT00", "XC00", "XT01", "XC01", "WC1V", "WC0S", "QX0", "QW1", "QW0", "H100", "H101", "AD",
+    "AM", "G100", "XT10", "G101", "XT11", "XC10", "H000", "QG0", "XC11", "H001", "BM", "BE",
+    "G000", "SM0", "QX1", "BI00", "SM1", "SE0", "G001", "H110", "SE1", "H111", "MK0", "G110",
+    "H010", "MK1", "H011", "G111", "XT20", "BI01", "XT21", "XC20", "QG1", "SM2", "G010", "XC21",
+    "SM3", "BI10", "SE2", "QX2", "SE3", "G011", "H120", "MK2", "H121", "G120", "MK3", "TR0",
+    "BI11", "G121", "TR1", "H020", "AS0", "H021", "XT30", "AS1", "XT31", "XC30", "TR2", "QG2",
+    "TR3", "G020", "XC31", "QX3", "BI20", "G021", "H130", "AS2", "BI21", "H131", "H030", "AS3",
+    "H031", "G130", "G131", "QA", "QG3", "G030", "AG00", "AG01", "G031", "BI30", "FI00", "FI01",
+    "ST00", "AG10", "BI31", "FI10", "ST01", "AG11", "FI11", "ST10", "AG20", "FI20", "ST11", "AG21",
+    "FI21", "ST20", "AG30", "FI30", "ST21", "AG31", "FI31", "ST30", "ST31",
+)
+
 
 def tile_modulatedgraphconv_pa_kernel(tc, x, W, M, adj, adj2, bias, out):
     nc = tc.nc
@@ -27,77 +41,30 @@ def tile_modulatedgraphconv_pa_kernel(tc, x, W, M, adj, adj2, bias, out):
         const = ctx.enter_context(tc.tile_pool(name="const", bufs=1))
         keep = ctx.enter_context(tc.tile_pool(name="keep", bufs=1))
         psum = ctx.enter_context(tc.psum_pool(name="psum", bufs=2))
+        if MANUAL:
+            ctx.enter_context(tc.manual_schedule())
 
         ident_f = const.tile([P, P], F32, name="ident_f")
-        make_identity(nc, ident_f[:])
-        warm_in = const.tile([P, 1], F32, name="warm_in")
-        nc.gpsimd.memset(warm_in[:], 0.0)
-        warm_out = const.tile([P, 1], F32, name="warm_out")
-        nc.scalar.activation(out=warm_out[:], in_=warm_in[:], func=ACT.Copy)
         ident_b = const.tile([P, P], BF16, name="ident_b")
-        make_identity(nc, ident_b[:])
         ones_b = const.tile([P, P], BF16, name="ones_b")
-        nc.gpsimd.memset(ones_b[:], 1.0)
         brow = const.tile([P, COUT], BF16, name="brow")
-        nc.gpsimd.memset(brow[:], 0.0)
         offmask = const.tile([P, P], F32, name="offmask")
-        nc.gpsimd.tensor_scalar(out=offmask[:], in0=ident_f[:], scalar1=-1.0, scalar2=1.0,
-                                op0=ALU.mult, op1=ALU.add)
+        warm_in = const.tile([P, 1], F32, name="warm_in")
+        warm_out = const.tile([P, 1], F32, name="warm_out")
 
-        w_raw = keep.tile([P, 4, 512], BF16, name="w_raw")
+        w_raw = [keep.tile([P, 2, 512], BF16, name="w_raw%d" % w) for w in range(2)]
         x_sb = [keep.tile([P, T * CIN], BF16, name="x_sb%d" % b) for b in range(B)]
         m_sb = keep.tile([P, T, COUT], BF16, name="m_sb")
         adj_sb = keep.tile([P, T, NODES], BF16, name="adj_sb")
         adj2_sb = keep.tile([P, T, NODES], BF16, name="adj2_sb")
         diag1 = keep.tile([P, T], BF16, name="diag1")
         diag2 = keep.tile([P, T], BF16, name="diag2")
-
-        def load_x(b):
-            nc.sync.dma_start(out=x_sb[b][:], in_=x[b].rearrange("(p t) k -> p (t k)", t=T))
-
-        nc.sync.dma_start(out=w_raw[:], in_=W.rearrange("w (u q e) c -> q (w u) (e c)", u=2, q=P, e=2))
-        load_x(0)
-        nc.sync.dma_start(out=m_sb[:], in_=M.rearrange("(p t) c -> p t c", t=T))
-        load_x(1)
-        nc.sync.dma_start(out=adj_sb[:], in_=adj.rearrange("(p t) i -> p t i", t=T))
-        nc.sync.dma_start(out=adj2_sb[:], in_=adj2.rearrange("(p t) i -> p t i", t=T))
-        load_x(2)
-        load_x(3)
-
-        nc.scalar.dma_start(out=brow[0:1, :], in_=bias.rearrange("(o c) -> o c", o=1))
-        with nc.allow_non_contiguous_dma(reason="the 512 diagonal elements, one piece each"):
-            nc.scalar.dma_start(
-                out=diag1[:],
-                in_=adj.rearrange("a b -> (a b)")[0:NODES * NODES:NODES + 1].rearrange("(p t) -> p t", t=T))
-            nc.scalar.dma_start(
-                out=diag2[:],
-                in_=adj2.rearrange("a b -> (a b)")[0:NODES * NODES:NODES + 1].rearrange("(p t) -> p t", t=T))
-
-        w_g = keep.tile([P, 2, 4 * COUT], BF16, name="w_g", align_bytes=64)
-        w_c = keep.tile([P, 2 * COUT], U32, name="w_c", align_bytes=64)
-        w_s = keep.tile([P, 2 * COUT], U8, name="w_s", align_bytes=64)
-        for w in (1, 0):
-            nc.vector.tensor_copy(
-                out=w_g[:, w, :].rearrange("p (c i s) -> p c s i", i=4, s=4),
-                in_=w_raw[:, 2 * w:2 * w + 2, :].rearrange("p u (e c i) -> p c (u e) i", e=2, i=4))
-        for w in (1, 0):
-            cols = slice(w * COUT, (w + 1) * COUT)
-            nc.vector.quantize_mx(out=w_c[:, cols].bitcast(FP8X4), scales=w_s[:, cols], in_=w_g[:, w, :])
-
-        bias_ps = psum.tile([P, COUT], F32, tag="agg", name="bias_ps")
-        nc.tensor.matmul(out=bias_ps[:], lhsT=ones_b[:], rhs=brow[:], start=True, stop=True)
+        w_g = [keep.tile([P, 4 * COUT], BF16, name="w_g%d" % w, align_bytes=64) for w in range(2)]
+        w_c = [keep.tile([P, COUT], U32, name="w_c%d" % w, align_bytes=64) for w in range(2)]
+        w_s = [keep.tile([P, COUT], U8, name="w_s%d" % w, align_bytes=64) for w in range(2)]
         bias2 = keep.tile([P, 2, COUT], F32, name="bias2")
-        for r in range(2):
-            nc.scalar.copy(out=bias2[:, r, :], in_=bias_ps[:])
         a_self = keep.tile([P, T], F32, name="a_self")
-        nc.gpsimd.tensor_tensor(out=a_self[:], in0=diag1[:], in1=diag2[:], op=ALU.add)
         a_m = keep.tile([P, T, COUT], F32, name="a_m")
-
-        def make_a_m():
-            for t in range(T):
-                nc.scalar.activation(out=a_m[:, t, :], in_=m_sb[:, t, :], func=ACT.Copy,
-                                     scale=a_self[:, t:t + 1])
-
         x_g = [keep.tile([P, T * P * 4], BF16, name="x_g%d" % b, align_bytes=64) for b in range(B)]
         x_c = [keep.tile([P, T * P], U32, name="x_c%d" % b, align_bytes=64) for b in range(B)]
         x_s = [keep.tile([P, T * P], U8, name="x_s%d" % b, align_bytes=64) for b in range(B)]
@@ -106,105 +73,201 @@ def tile_modulatedgraphconv_pa_kernel(tc, x, W, M, adj, adj2, bias, out):
         g_s = [keep.tile([P, COUT], U8, name="g_s%d" % b, align_bytes=64) for b in range(B)]
         g0 = [keep.tile([P, T, COUT], F32, name="g0_%d" % b) for b in range(B)]
         o_sb = [keep.tile([P, T, COUT], F32, name="o_sb%d" % b) for b in range(B)]
-
-        def transpose_x(b):
-            xw = x_sb[b][:].bitcast(F32)
-            gw = x_g[b][:].bitcast(F32).rearrange("p (t n u) -> p t n u", t=T, u=2)
-            for h in range(2):
-                xt = psum.tile([P, 2, 2, P], F32, tag="xt", name="xt_%d_%d" % (b, h))
-                for tt in range(2):
-                    for u in range(2):
-                        c0 = (2 * h + tt) * 256 + u * P
-                        nc.tensor.transpose(xt[:, tt, u, :], xw[:, c0:c0 + P], ident_f[:])
-                nc.scalar.copy(out=gw[:, 2 * h:2 * h + 2, :, :], in_=xt[:].rearrange("p t u n -> p t n u"))
-
-        def quantise_x(b):
-            nc.vector.quantize_mx(out=x_c[b][:].bitcast(FP8X4), scales=x_s[b][:], in_=x_g[b][:])
-
-        def stage1(b):
-            gv = g_g[b][:].rearrange("p (c t) -> p c t", t=T)
-            for ch in range(2):
-                h1 = psum.tile([P, T, P], F32, tag="h1", name="h1_%d_%d" % (b, ch))
-                wc = slice(COUT + ch * P, COUT + (ch + 1) * P)
-                for t in range(T):
-                    nodes = slice(t * P, (t + 1) * P)
-                    nc.tensor.matmul_mx(out=h1[:, t, :],
-                                        lhsT=x_c[b][:, nodes].bitcast(FP8X4), lhsT_scale=x_s[b][:, nodes],
-                                        rhs=w_c[:, wc].bitcast(FP8X4), rhs_scale=w_s[:, wc],
-                                        start=True, stop=True)
-                cc = slice(ch * P, (ch + 1) * P)
-                nc.vector.tensor_tensor(out=gv[:, cc, :], in0=h1[:].rearrange("p t c -> p c t"),
-                                        in1=m_sb[:, :, cc].rearrange("p t c -> p c t"), op=ALU.mult)
-            nc.vector.quantize_mx(out=g_c[b][:].bitcast(FP8X4), scales=g_s[b][:], in_=g_g[b][:])
-            for h in range(2):
-                h0 = psum.tile([P, 2, COUT], F32, tag="h0", name="h0_%d_%d" % (b, h))
-                for tt in range(2):
-                    nodes = slice((2 * h + tt) * P, (2 * h + tt + 1) * P)
-                    nc.tensor.matmul_mx(out=h0[:, tt, :],
-                                        lhsT=x_c[b][:, nodes].bitcast(FP8X4), lhsT_scale=x_s[b][:, nodes],
-                                        rhs=w_c[:, 0:COUT].bitcast(FP8X4), rhs_scale=w_s[:, 0:COUT],
-                                        start=True, stop=True)
-                ts = slice(2 * h, 2 * h + 2)
-                nc.vector.tensor_tensor(out=g0[b][:, ts, :], in0=h0[:], in1=a_m[:, ts, :], op=ALU.mult)
-                nc.gpsimd.tensor_tensor(out=g0[b][:, ts, :], in0=g0[b][:, ts, :], in1=bias2[:], op=ALU.add)
-
         s_perm = keep.tile([P, T, NODES], F32, name="s_perm")
         a_g = keep.tile([P, NODES * 4], BF16, name="a_g", align_bytes=64)
         a_c = keep.tile([P, NODES], U32, name="a_c", align_bytes=64)
         a_s = keep.tile([P, NODES], U8, name="a_s", align_bytes=64)
+        live = {}
 
-        def a_sum_rows():
+        def load_x_half(b, h):
+            nc.sync.dma_start(out=x_sb[b][:, 2 * h * CIN:(2 * h + 2) * CIN].rearrange("p (t k) -> p t k", t=2),
+                              in_=x[b].rearrange("(p t) k -> p t k", t=T)[:, 2 * h:2 * h + 2, :])
+
+        def load_x(b):
+            nc.sync.dma_start(out=x_sb[b][:], in_=x[b].rearrange("(p t) k -> p (t k)", t=T))
+
+        def load_w(w):
+            nc.sync.dma_start(out=w_raw[w][:], in_=W[w].rearrange("(u q e) c -> q u (e c)", u=2, q=P, e=2))
+
+        def small_loads():
+            nc.scalar.dma_start(out=brow[0:1, :], in_=bias.rearrange("(o c) -> o c", o=1))
+            with nc.allow_non_contiguous_dma(reason="the 512 diagonal elements, one piece each"):
+                nc.scalar.dma_start(
+                    out=diag1[:],
+                    in_=adj.rearrange("a b -> (a b)")[0:NODES * NODES:NODES + 1].rearrange("(p t) -> p t", t=T))
+                nc.scalar.dma_start(
+                    out=diag2[:],
+                    in_=adj2.rearrange("a b -> (a b)")[0:NODES * NODES:NODES + 1].rearrange("(p t) -> p t", t=T))
+
+        def consts():
+            make_identity(nc, ident_f[:])
+            nc.gpsimd.memset(warm_in[:], 0.0)
+            nc.gpsimd.memset(brow[:], 0.0)
+            nc.gpsimd.memset(ones_b[:], 1.0)
+            make_identity(nc, ident_b[:])
+            nc.gpsimd.tensor_scalar(out=offmask[:], in0=ident_f[:], scalar1=-1.0, scalar2=1.0,
+                                    op0=ALU.mult, op1=ALU.add)
+
+        def op_WC(w, eng):
+            dst = w_g[w][:].rearrange("p (c i s) -> p c s i", i=4, s=4)
+            src = w_raw[w][:].rearrange("p u (e c i) -> p c (u e) i", e=2, i=4)
+            if eng == "V":
+                nc.vector.tensor_copy(out=dst, in_=src)
+            else:
+                nc.scalar.copy(out=dst, in_=src)
+
+        def op_QW(w):
+            nc.vector.quantize_mx(out=w_c[w][:].bitcast(FP8X4), scales=w_s[w][:], in_=w_g[w][:])
+
+        def op_BM():
+            bias_ps = psum.tile([P, COUT], F32, tag="agg", name="bias_ps")
+            nc.tensor.matmul(out=bias_ps[:], lhsT=ones_b[:], rhs=brow[:], start=True, stop=True)
+            live["bias"] = bias_ps
+
+        def op_BE():
+            for r in range(2):
+                nc.scalar.copy(out=bias2[:, r, :], in_=live["bias"][:])
+
+        def op_AD():
+            nc.gpsimd.tensor_tensor(out=a_self[:], in0=diag1[:], in1=diag2[:], op=ALU.add)
+
+        def op_AM():
             for t in range(T):
-                s_ps = psum.tile([P, NODES], F32, tag="agg", name="s_ps%d" % t)
-                nc.tensor.matmul(out=s_ps[:], lhsT=ident_b[:], rhs=adj_sb[:, t, :], start=True, stop=False)
-                nc.tensor.matmul(out=s_ps[:], lhsT=ident_b[:], rhs=adj2_sb[:, t, :], start=False, stop=True)
-                nc.scalar.activation(out=s_perm[:, t, :].rearrange("p (s c) -> p s c", s=T),
-                                     in_=s_ps[:].rearrange("p (c s) -> p s c", s=T),
-                                     func=ACT.Copy, scale=0.5)
-                blk = s_perm[:, t, t * P:(t + 1) * P]
-                nc.gpsimd.tensor_tensor(out=blk, in0=blk, in1=offmask[:], op=ALU.mult)
+                nc.gpsimd.tensor_scalar(out=a_m[:, t, :], in0=m_sb[:, t, :], scalar1=a_self[:, t:t + 1],
+                                        scalar2=0.0, op0=ALU.mult, op1=ALU.add)
 
-        def a_symmetrise():
+        def op_XT(b, h):
+            xw = x_sb[b][:, 2 * h * CIN:(2 * h + 2) * CIN].bitcast(F32)
+            xt = psum.tile([P, 2, 2, P], F32, tag="xt", name="xt_%d_%d" % (b, h))
+            for tt in range(2):
+                for u in range(2):
+                    c0 = tt * 256 + u * P
+                    nc.tensor.transpose(xt[:, tt, u, :], xw[:, c0:c0 + P], ident_f[:])
+            live["xt", b, h] = xt
+
+        def op_XC(b, h):
+            gw = x_g[b][:].bitcast(F32).rearrange("p (t n u) -> p t n u", t=T, u=2)
+            nc.scalar.copy(out=gw[:, 2 * h:2 * h + 2, :, :],
+                           in_=live["xt", b, h][:].rearrange("p t u n -> p t n u"))
+
+        def op_QX(b):
+            nc.vector.quantize_mx(out=x_c[b][:].bitcast(FP8X4), scales=x_s[b][:], in_=x_g[b][:])
+
+        def op_H1(b, ch):
+            h1 = psum.tile([P, T, P], F32, tag="h1", name="h1_%d_%d" % (b, ch))
+            wc = slice(ch * P, (ch + 1) * P)
+            for t in range(T):
+                nodes = slice(t * P, (t + 1) * P)
+                nc.tensor.matmul_mx(out=h1[:, t, :],
+                                    lhsT=x_c[b][:, nodes].bitcast(FP8X4), lhsT_scale=x_s[b][:, nodes],
+                                    rhs=w_c[1][:, wc].bitcast(FP8X4), rhs_scale=w_s[1][:, wc],
+                                    start=True, stop=True)
+            live["h1", b, ch] = h1
+
+        def op_G1(b, ch):
+            gv = g_g[b][:].rearrange("p (c t) -> p c t", t=T)
+            cc = slice(ch * P, (ch + 1) * P)
+            nc.vector.tensor_tensor(out=gv[:, cc, :], in0=live["h1", b, ch][:].rearrange("p t c -> p c t"),
+                                    in1=m_sb[:, :, cc].rearrange("p t c -> p c t"), op=ALU.mult)
+
+        def op_QG(b):
+            nc.vector.quantize_mx(out=g_c[b][:].bitcast(FP8X4), scales=g_s[b][:], in_=g_g[b][:])
+
+        def op_H0(b, h):
+            h0 = psum.tile([P, 2, COUT], F32, tag="h0", name="h0_%d_%d" % (b, h))
+            for tt in range(2):
+                nodes = slice((2 * h + tt) * P, (2 * h + tt + 1) * P)
+                nc.tensor.matmul_mx(out=h0[:, tt, :],
+                                    lhsT=x_c[b][:, nodes].bitcast(FP8X4), lhsT_scale=x_s[b][:, nodes],
+                                    rhs=w_c[0][:].bitcast(FP8X4), rhs_scale=w_s[0][:],
+                                    start=True, stop=True)
+            live["h0", b, h] = h0
+
+        def op_G0(b, h):
+            ts = slice(2 * h, 2 * h + 2)
+            nc.vector.tensor_tensor(out=g0[b][:, ts, :], in0=live["h0", b, h][:], in1=a_m[:, ts, :], op=ALU.mult)
+
+        def op_E0(b, h):
+            ts = slice(2 * h, 2 * h + 2)
+            nc.scalar.copy(out=g0[b][:, ts, :], in_=live["h0", b, h][:])
+
+        def op_P0(b, h):
+            ts = slice(2 * h, 2 * h + 2)
+            nc.gpsimd.tensor_tensor(out=g0[b][:, ts, :], in0=g0[b][:, ts, :], in1=a_m[:, ts, :], op=ALU.mult)
+
+        def op_BI(b, h):
+            ts = slice(2 * h, 2 * h + 2)
+            nc.gpsimd.tensor_tensor(out=g0[b][:, ts, :], in0=g0[b][:, ts, :], in1=bias2[:], op=ALU.add)
+
+        def op_SM(t):
+            s_ps = psum.tile([P, NODES], F32, tag="agg", name="s_ps%d" % t)
+            nc.tensor.matmul(out=s_ps[:], lhsT=ident_b[:], rhs=adj_sb[:, t, :], start=True, stop=False)
+            nc.tensor.matmul(out=s_ps[:], lhsT=ident_b[:], rhs=adj2_sb[:, t, :], start=False, stop=True)
+            live["s", t] = s_ps
+
+        def op_SE(t):
+            nc.scalar.activation(out=s_perm[:, t, :].rearrange("p (s c) -> p s c", s=T),
+                                 in_=live["s", t][:].rearrange("p (c s) -> p s c", s=T),
+                                 func=ACT.Copy, scale=0.5)
+
+        def op_MK(t):
+            blk = s_perm[:, t, t * P:(t + 1) * P]
+            nc.gpsimd.tensor_tensor(out=blk, in0=blk, in1=offmask[:], op=ALU.mult)
+
+        def op_TR(tp):
+            tr = psum.tile([P, T, P], F32, tag="agg", name="tr%d" % tp)
+            for t in range(T):
+                nc.tensor.transpose(tr[:, t, :], s_perm[:, tp, t * P:(t + 1) * P], ident_f[:])
+            live["tr", tp] = tr
+
+        def op_AS(tp):
             av = a_g[:].rearrange("p (c t) -> p c t", t=T)
-            for tp in range(T):
-                tr = psum.tile([P, T, P], F32, tag="agg", name="tr%d" % tp)
-                for t in range(T):
-                    nc.tensor.transpose(tr[:, t, :], s_perm[:, tp, t * P:(t + 1) * P], ident_f[:])
-                cc = slice(tp * P, (tp + 1) * P)
-                nc.vector.tensor_tensor(out=av[:, cc, :], in0=tr[:].rearrange("p t c -> p c t"),
-                                        in1=s_perm[:, :, cc].rearrange("p t c -> p c t"), op=ALU.add)
+            cc = slice(tp * P, (tp + 1) * P)
+            nc.vector.tensor_tensor(out=av[:, cc, :], in0=live["tr", tp][:].rearrange("p t c -> p c t"),
+                                    in1=s_perm[:, :, cc].rearrange("p t c -> p c t"), op=ALU.add)
+
+        def op_QA():
             nc.vector.quantize_mx(out=a_c[:].bitcast(FP8X4), scales=a_s[:], in_=a_g[:])
 
-        def stage2(b):
-            ov = out[b].rearrange("(p t) c -> p t c", t=T)
-            for h in range(2):
-                agg = psum.tile([P, 2, COUT], F32, tag="agg", name="agg_%d_%d" % (b, h))
-                for tt in range(2):
-                    rows = slice((2 * h + tt) * P, (2 * h + tt + 1) * P)
-                    nc.tensor.matmul_mx(out=agg[:, tt, :],
-                                        lhsT=a_c[:, rows].bitcast(FP8X4), lhsT_scale=a_s[:, rows],
-                                        rhs=g_c[b][:].bitcast(FP8X4), rhs_scale=g_s[b][:],
-                                        start=True, stop=True)
-                ts = slice(2 * h, 2 * h + 2)
-                nc.vector.tensor_tensor(out=o_sb[b][:, ts, :], in0=agg[:], in1=g0[b][:, ts, :], op=ALU.add)
-                nc.sync.dma_start(out=ov[:, ts, :], in_=o_sb[b][:, ts, :])
+        def op_AG(b, h):
+            agg = psum.tile([P, 2, COUT], F32, tag="agg", name="agg_%d_%d" % (b, h))
+            for tt in range(2):
+                rows = slice((2 * h + tt) * P, (2 * h + tt + 1) * P)
+                nc.tensor.matmul_mx(out=agg[:, tt, :],
+                                    lhsT=a_c[:, rows].bitcast(FP8X4), lhsT_scale=a_s[:, rows],
+                                    rhs=g_c[b][:].bitcast(FP8X4), rhs_scale=g_s[b][:],
+                                    start=True, stop=True)
+            live["agg", b, h] = agg
 
-        transpose_x(0)
-        make_a_m()
-        quantise_x(0)
-        transpose_x(1)
-        stage1(0)
-        quantise_x(1)
-        a_sum_rows()
-        stage1(1)
-        transpose_x(2)
-        a_symmetrise()
-        quantise_x(2)
-        stage2(0)
-        stage1(2)
-        transpose_x(3)
-        stage2(1)
-        quantise_x(3)
-        stage1(3)
-        stage2(2)
-        stage2(3)
+        def op_FI(b, h):
+            ts = slice(2 * h, 2 * h + 2)
+            nc.vector.tensor_tensor(out=o_sb[b][:, ts, :], in0=live["agg", b, h][:], in1=g0[b][:, ts, :], op=ALU.add)
+
+        def op_ST(b, h):
+            ts = slice(2 * h, 2 * h + 2)
+            nc.sync.dma_start(out=out[b].rearrange("(p t) c -> p t c", t=T)[:, ts, :], in_=o_sb[b][:, ts, :])
+
+        ops = {"XT": op_XT, "XC": op_XC, "QX": op_QX, "H1": op_H1, "G1": op_G1, "QG": op_QG, "H0": op_H0,
+               "G0": op_G0, "E0": op_E0, "P0": op_P0, "BI": op_BI, "SM": op_SM, "SE": op_SE, "MK": op_MK,
+               "TR": op_TR, "AS": op_AS, "QA": op_QA, "AG": op_AG, "FI": op_FI, "ST": op_ST, "QW": op_QW,
+               "BM": op_BM, "BE": op_BE, "AD": op_AD, "AM": op_AM}
+
+        consts()
+        nc.scalar.activation(out=warm_out[:], in_=warm_in[:], func=ACT.Copy)
+        small_loads()
+        load_x_half(0, 0)
+        load_x_half(0, 1)
+        load_w(1)
+        load_w(0)
+        load_x(1)
+        nc.sync.dma_start(out=m_sb[:], in_=M.rearrange("(p t) c -> p t c", t=T))
+        nc.sync.dma_start(out=adj_sb[:], in_=adj.rearrange("(p t) i -> p t i", t=T))
+        nc.sync.dma_start(out=adj2_sb[:], in_=adj2.rearrange("(p t) i -> p t i", t=T))
+        load_x(2)
+        load_x(3)
+        for word in ORDER:
+            kind = word[0:2]
+            if kind == "WC":
+                op_WC(int(word[2]), word[3])
+            else:
+                ops[kind](*[int(d) for d in word[2:]])

@@ -22,16 +22,16 @@ T = 4
 
 MANUAL = True
 ORDER = (
-    "XT00", "XC00", "XT01", "XC01", "WC1V", "WC0S", "QX0", "QW1", "QW0", "H100", "H101", "AD",
-    "AM", "G100", "XT10", "G101", "XT11", "XC10", "H000", "QG0", "XC11", "H001", "BM", "BE",
-    "G000", "SM0", "QX1", "BI00", "SM1", "SE0", "G001", "H110", "SE1", "H111", "MK0", "G110",
-    "H010", "MK1", "H011", "G111", "XT20", "BI01", "XT21", "XC20", "QG1", "SM2", "G010", "XC21",
-    "SM3", "BI10", "SE2", "QX2", "SE3", "G011", "H120", "MK2", "H121", "G120", "MK3", "TR0",
-    "BI11", "G121", "TR1", "H020", "AS0", "H021", "XT30", "AS1", "XT31", "XC30", "TR2", "QG2",
-    "TR3", "G020", "XC31", "QX3", "BI20", "G021", "H130", "AS2", "BI21", "H131", "H030", "AS3",
-    "H031", "G130", "G131", "QA", "QG3", "G030", "AG00", "AG01", "G031", "BI30", "FI00", "FI01",
-    "ST00", "AG10", "BI31", "FI10", "ST01", "AG11", "FI11", "ST10", "AG20", "FI20", "ST11", "AG21",
-    "FI21", "ST20", "AG30", "FI30", "ST21", "AG31", "FI31", "ST30", "ST31",
+    "XT00", "XT01", "XC00", "WC1V", "XC01", "QW1", "AD", "BM", "WC0S", "QX0", "XT10", "AM",
+    "XT11", "QW0", "XC10", "H100", "H101", "XC11", "H000", "G100", "H001", "BE", "XT20", "G101",
+    "XT21", "QX1", "XC20", "QG0", "G000", "XC21", "H110", "G001", "H111", "BI00", "XT30", "QX2",
+    "XT31", "G110", "XC30", "H010", "G111", "H011", "BI01", "XC31", "SM0", "QG1", "G010", "SM1",
+    "SE0", "G011", "H120", "H121", "SE1", "QX3", "SM2", "MK0", "G120", "SM3", "MK1", "SE2",
+    "G121", "H020", "BI10", "H021", "SE3", "QG2", "TR0", "G020", "TR1", "G021", "H130", "MK2",
+    "H131", "MK3", "G130", "TR2", "BI11", "G131", "TR3", "AS0", "H030", "AS1", "H031", "BI20",
+    "QG3", "AS2", "AS3", "BI21", "QA", "G030", "G031", "AG00", "AG01", "BI30", "AG10", "FI00",
+    "AG11", "AG20", "FI01", "AG21", "ST00", "AG30", "FI10", "BI31", "AG31", "ST01", "FI11", "ST10",
+    "FI20", "ST11", "FI21", "ST20", "FI30", "ST21", "FI31", "ST30", "ST31",
 )
 
 
@@ -40,7 +40,7 @@ def tile_modulatedgraphconv_pa_kernel(tc, x, W, M, adj, adj2, bias, out):
     with ExitStack() as ctx:
         const = ctx.enter_context(tc.tile_pool(name="const", bufs=1))
         keep = ctx.enter_context(tc.tile_pool(name="keep", bufs=1))
-        psum = ctx.enter_context(tc.psum_pool(name="psum", bufs=2))
+        psum = ctx.enter_context(tc.psum_pool(name="psum", bufs=1))
         if MANUAL:
             ctx.enter_context(tc.manual_schedule())
 
@@ -71,8 +71,8 @@ def tile_modulatedgraphconv_pa_kernel(tc, x, W, M, adj, adj2, bias, out):
         g_g = [keep.tile([P, COUT * 4], BF16, name="g_g%d" % b, align_bytes=64) for b in range(B)]
         g_c = [keep.tile([P, COUT], U32, name="g_c%d" % b, align_bytes=64) for b in range(B)]
         g_s = [keep.tile([P, COUT], U8, name="g_s%d" % b, align_bytes=64) for b in range(B)]
-        g0 = [keep.tile([P, T, COUT], F32, name="g0_%d" % b) for b in range(B)]
-        o_sb = [keep.tile([P, T, COUT], F32, name="o_sb%d" % b) for b in range(B)]
+        g0 = [[keep.tile([P, 2, COUT], F32, name="g0_%d_%d" % (b, h)) for h in range(2)] for b in range(B)]
+        o_sb = [[keep.tile([P, 2, COUT], F32, name="o_sb%d_%d" % (b, h)) for h in range(2)] for b in range(B)]
         s_perm = keep.tile([P, T, NODES], F32, name="s_perm")
         a_g = keep.tile([P, NODES * 4], BF16, name="a_g", align_bytes=64)
         a_c = keep.tile([P, NODES], U32, name="a_c", align_bytes=64)
@@ -90,12 +90,12 @@ def tile_modulatedgraphconv_pa_kernel(tc, x, W, M, adj, adj2, bias, out):
             nc.sync.dma_start(out=w_raw[w][:], in_=W[w].rearrange("(u q e) c -> q u (e c)", u=2, q=P, e=2))
 
         def small_loads():
-            nc.scalar.dma_start(out=brow[0:1, :], in_=bias.rearrange("(o c) -> o c", o=1))
+            nc.sync.dma_start(out=brow[0:1, :], in_=bias.rearrange("(o c) -> o c", o=1))
             with nc.allow_non_contiguous_dma(reason="the 512 diagonal elements, one piece each"):
-                nc.scalar.dma_start(
+                nc.sync.dma_start(
                     out=diag1[:],
                     in_=adj.rearrange("a b -> (a b)")[0:NODES * NODES:NODES + 1].rearrange("(p t) -> p t", t=T))
-                nc.scalar.dma_start(
+                nc.sync.dma_start(
                     out=diag2[:],
                     in_=adj2.rearrange("a b -> (a b)")[0:NODES * NODES:NODES + 1].rearrange("(p t) -> p t", t=T))
 
@@ -120,7 +120,7 @@ def tile_modulatedgraphconv_pa_kernel(tc, x, W, M, adj, adj2, bias, out):
             nc.vector.quantize_mx(out=w_c[w][:].bitcast(FP8X4), scales=w_s[w][:], in_=w_g[w][:])
 
         def op_BM():
-            bias_ps = psum.tile([P, COUT], F32, tag="agg", name="bias_ps")
+            bias_ps = psum.tile([P, COUT], F32, tag="aa0", name="bias_ps")
             nc.tensor.matmul(out=bias_ps[:], lhsT=ones_b[:], rhs=brow[:], start=True, stop=True)
             live["bias"] = bias_ps
 
@@ -138,7 +138,7 @@ def tile_modulatedgraphconv_pa_kernel(tc, x, W, M, adj, adj2, bias, out):
 
         def op_XT(b, h):
             xw = x_sb[b][:, 2 * h * CIN:(2 * h + 2) * CIN].bitcast(F32)
-            xt = psum.tile([P, 2, 2, P], F32, tag="xt", name="xt_%d_%d" % (b, h))
+            xt = psum.tile([P, 2, 2, P], F32, tag=("aa" if b == 3 else "xt") + str(h), name="xt_%d_%d" % (b, h))
             for tt in range(2):
                 for u in range(2):
                     c0 = tt * 256 + u * P
@@ -154,7 +154,7 @@ def tile_modulatedgraphconv_pa_kernel(tc, x, W, M, adj, adj2, bias, out):
             nc.vector.quantize_mx(out=x_c[b][:].bitcast(FP8X4), scales=x_s[b][:], in_=x_g[b][:])
 
         def op_H1(b, ch):
-            h1 = psum.tile([P, T, P], F32, tag="h1", name="h1_%d_%d" % (b, ch))
+            h1 = psum.tile([P, T, P], F32, tag="h1" + str(ch), name="h1_%d_%d" % (b, ch))
             wc = slice(ch * P, (ch + 1) * P)
             for t in range(T):
                 nodes = slice(t * P, (t + 1) * P)
@@ -174,7 +174,7 @@ def tile_modulatedgraphconv_pa_kernel(tc, x, W, M, adj, adj2, bias, out):
             nc.vector.quantize_mx(out=g_c[b][:].bitcast(FP8X4), scales=g_s[b][:], in_=g_g[b][:])
 
         def op_H0(b, h):
-            h0 = psum.tile([P, 2, COUT], F32, tag="h0", name="h0_%d_%d" % (b, h))
+            h0 = psum.tile([P, 2, COUT], F32, tag="h0" + str(h), name="h0_%d_%d" % (b, h))
             for tt in range(2):
                 nodes = slice((2 * h + tt) * P, (2 * h + tt + 1) * P)
                 nc.tensor.matmul_mx(out=h0[:, tt, :],
@@ -185,22 +185,22 @@ def tile_modulatedgraphconv_pa_kernel(tc, x, W, M, adj, adj2, bias, out):
 
         def op_G0(b, h):
             ts = slice(2 * h, 2 * h + 2)
-            nc.vector.tensor_tensor(out=g0[b][:, ts, :], in0=live["h0", b, h][:], in1=a_m[:, ts, :], op=ALU.mult)
+            nc.vector.tensor_tensor(out=g0[b][h][:], in0=live["h0", b, h][:], in1=a_m[:, ts, :], op=ALU.mult)
 
         def op_E0(b, h):
             ts = slice(2 * h, 2 * h + 2)
-            nc.scalar.copy(out=g0[b][:, ts, :], in_=live["h0", b, h][:])
+            nc.scalar.copy(out=g0[b][h][:], in_=live["h0", b, h][:])
 
         def op_P0(b, h):
             ts = slice(2 * h, 2 * h + 2)
-            nc.gpsimd.tensor_tensor(out=g0[b][:, ts, :], in0=g0[b][:, ts, :], in1=a_m[:, ts, :], op=ALU.mult)
+            nc.gpsimd.tensor_tensor(out=g0[b][h][:], in0=g0[b][h][:], in1=a_m[:, ts, :], op=ALU.mult)
 
         def op_BI(b, h):
             ts = slice(2 * h, 2 * h + 2)
-            nc.gpsimd.tensor_tensor(out=g0[b][:, ts, :], in0=g0[b][:, ts, :], in1=bias2[:], op=ALU.add)
+            nc.gpsimd.tensor_tensor(out=g0[b][h][:], in0=g0[b][h][:], in1=bias2[:], op=ALU.add)
 
         def op_SM(t):
-            s_ps = psum.tile([P, NODES], F32, tag="agg", name="s_ps%d" % t)
+            s_ps = psum.tile([P, NODES], F32, tag=("xt" if t < 2 else "aa") + str(t % 2), name="s_ps%d" % t)
             nc.tensor.matmul(out=s_ps[:], lhsT=ident_b[:], rhs=adj_sb[:, t, :], start=True, stop=False)
             nc.tensor.matmul(out=s_ps[:], lhsT=ident_b[:], rhs=adj2_sb[:, t, :], start=False, stop=True)
             live["s", t] = s_ps
@@ -215,7 +215,7 @@ def tile_modulatedgraphconv_pa_kernel(tc, x, W, M, adj, adj2, bias, out):
             nc.gpsimd.tensor_tensor(out=blk, in0=blk, in1=offmask[:], op=ALU.mult)
 
         def op_TR(tp):
-            tr = psum.tile([P, T, P], F32, tag="agg", name="tr%d" % tp)
+            tr = psum.tile([P, T, P], F32, tag=("xt" if tp < 2 else "aa") + str(tp % 2), name="tr%d" % tp)
             for t in range(T):
                 nc.tensor.transpose(tr[:, t, :], s_perm[:, tp, t * P:(t + 1) * P], ident_f[:])
             live["tr", tp] = tr
@@ -230,7 +230,7 @@ def tile_modulatedgraphconv_pa_kernel(tc, x, W, M, adj, adj2, bias, out):
             nc.vector.quantize_mx(out=a_c[:].bitcast(FP8X4), scales=a_s[:], in_=a_g[:])
 
         def op_AG(b, h):
-            agg = psum.tile([P, 2, COUT], F32, tag="agg", name="agg_%d_%d" % (b, h))
+            agg = psum.tile([P, 2, COUT], F32, tag=("xt", "aa", "h1", "h0")[b] + str(h), name="agg_%d_%d" % (b, h))
             for tt in range(2):
                 rows = slice((2 * h + tt) * P, (2 * h + tt + 1) * P)
                 nc.tensor.matmul_mx(out=agg[:, tt, :],
@@ -241,11 +241,11 @@ def tile_modulatedgraphconv_pa_kernel(tc, x, W, M, adj, adj2, bias, out):
 
         def op_FI(b, h):
             ts = slice(2 * h, 2 * h + 2)
-            nc.vector.tensor_tensor(out=o_sb[b][:, ts, :], in0=live["agg", b, h][:], in1=g0[b][:, ts, :], op=ALU.add)
+            nc.vector.tensor_tensor(out=o_sb[b][h][:], in0=live["agg", b, h][:], in1=g0[b][h][:], op=ALU.add)
 
         def op_ST(b, h):
             ts = slice(2 * h, 2 * h + 2)
-            nc.sync.dma_start(out=out[b].rearrange("(p t) c -> p t c", t=T)[:, ts, :], in_=o_sb[b][:, ts, :])
+            nc.sync.dma_start(out=out[b].rearrange("(p t) c -> p t c", t=T)[:, ts, :], in_=o_sb[b][h][:])
 
         ops = {"XT": op_XT, "XC": op_XC, "QX": op_QX, "H1": op_H1, "G1": op_G1, "QG": op_QG, "H0": op_H0,
                "G0": op_G0, "E0": op_E0, "P0": op_P0, "BI": op_BI, "SM": op_SM, "SE": op_SE, "MK": op_MK,
@@ -254,17 +254,17 @@ def tile_modulatedgraphconv_pa_kernel(tc, x, W, M, adj, adj2, bias, out):
 
         consts()
         nc.scalar.activation(out=warm_out[:], in_=warm_in[:], func=ACT.Copy)
-        small_loads()
         load_x_half(0, 0)
         load_x_half(0, 1)
         load_w(1)
         load_w(0)
+        small_loads()
         load_x(1)
         nc.sync.dma_start(out=m_sb[:], in_=M.rearrange("(p t) c -> p t c", t=T))
-        nc.sync.dma_start(out=adj_sb[:], in_=adj.rearrange("(p t) i -> p t i", t=T))
-        nc.sync.dma_start(out=adj2_sb[:], in_=adj2.rearrange("(p t) i -> p t i", t=T))
         load_x(2)
         load_x(3)
+        nc.sync.dma_start(out=adj_sb[:], in_=adj.rearrange("(p t) i -> p t i", t=T))
+        nc.sync.dma_start(out=adj2_sb[:], in_=adj2.rearrange("(p t) i -> p t i", t=T))
         for word in ORDER:
             kind = word[0:2]
             if kind == "WC":

@@ -22,16 +22,16 @@ T = 4
 
 MANUAL = True
 ORDER = (
-    "XT00", "XT01", "XC00", "WC1V", "XC01", "QW1", "AD", "BM", "WC0S", "QX0", "XT10", "AM",
-    "XT11", "QW0", "XC10", "H100", "H101", "XC11", "H000", "G100", "H001", "BE", "XT20", "G101",
-    "XT21", "QX1", "XC20", "QG0", "G000", "XC21", "H110", "G001", "H111", "BI00", "XT30", "QX2",
-    "XT31", "G110", "XC30", "H010", "G111", "H011", "BI01", "XC31", "SM0", "QG1", "G010", "SM1",
-    "SE0", "G011", "H120", "H121", "SE1", "QX3", "SM2", "MK0", "G120", "SM3", "MK1", "SE2",
-    "G121", "H020", "BI10", "H021", "SE3", "QG2", "TR0", "G020", "TR1", "G021", "H130", "MK2",
-    "H131", "MK3", "G130", "TR2", "BI11", "G131", "TR3", "AS0", "H030", "AS1", "H031", "BI20",
-    "QG3", "AS2", "AS3", "BI21", "QA", "G030", "G031", "AG00", "AG01", "BI30", "AG10", "FI00",
-    "AG11", "AG20", "FI01", "AG21", "ST00", "AG30", "FI10", "BI31", "AG31", "ST01", "FI11", "ST10",
-    "FI20", "ST11", "FI21", "ST20", "FI30", "ST21", "FI31", "ST30", "ST31",
+    "XT00", "XT01", "XC00", "WC1V", "XC01", "QW1", "WC0S", "QX0", "XT10", "XT11", "AD", "QW0",
+    "AM", "XC10", "BM", "H100", "XC11", "H101", "H000", "G100", "BE", "H001", "XT20", "G101",
+    "XT21", "QX1", "XC20", "XT30", "G000", "XC21", "G001", "H110", "XT31", "BI00", "XC30", "G110",
+    "H111", "H010", "XC31", "SM0", "G111", "BI01", "SM1", "QY", "SE0", "H011", "SM2", "SE1",
+    "G010", "MK0", "SE2", "G011", "H120", "MK1", "H121", "BI10", "SM3", "G120", "H020", "G121",
+    "H021", "SE3", "H130", "G020", "MK2", "H131", "G021", "TR0", "MK3", "G130", "TR1", "BI11",
+    "G131", "TR2", "QH", "TR3", "BI20", "H030", "H031", "AS0", "AS1", "AS2", "BI21", "AS3",
+    "QA", "G030", "G031", "AG00", "AG01", "BI30", "AG10", "FI00", "AG11", "AG20", "FI01", "AG21",
+    "ST00", "AG30", "FI10", "BI31", "AG31", "ST01", "FI11", "ST10", "FI20", "ST11", "FI21", "ST20",
+    "FI30", "ST21", "FI31", "ST30", "ST31",
 )
 
 
@@ -65,12 +65,18 @@ def tile_modulatedgraphconv_pa_kernel(tc, x, W, M, adj, adj2, bias, out):
         bias2 = keep.tile([P, 2, COUT], F32, name="bias2")
         a_self = keep.tile([P, T], F32, name="a_self")
         a_m = keep.tile([P, T, COUT], F32, name="a_m")
-        x_g = [keep.tile([P, T * P * 4], BF16, name="x_g%d" % b, align_bytes=64) for b in range(B)]
-        x_c = [keep.tile([P, T * P], U32, name="x_c%d" % b, align_bytes=64) for b in range(B)]
-        x_s = [keep.tile([P, T * P], U8, name="x_s%d" % b, align_bytes=64) for b in range(B)]
-        g_g = [keep.tile([P, COUT * 4], BF16, name="g_g%d" % b, align_bytes=64) for b in range(B)]
-        g_c = [keep.tile([P, COUT], U32, name="g_c%d" % b, align_bytes=64) for b in range(B)]
-        g_s = [keep.tile([P, COUT], U8, name="g_s%d" % b, align_bytes=64) for b in range(B)]
+        xg_t = [keep.tile([P, n * T * P * 4], BF16, name="xg_t%d" % i, align_bytes=64) for i, n in enumerate((1, 1, 2))]
+        xc_t = [keep.tile([P, n * T * P], U32, name="xc_t%d" % i, align_bytes=64) for i, n in enumerate((1, 1, 2))]
+        xs_t = [keep.tile([P, n * T * P], U8, name="xs_t%d" % i, align_bytes=64) for i, n in enumerate((1, 1, 2))]
+        x_g = [xg_t[min(b, 2)][:, max(b - 2, 0) * T * P * 4:(max(b - 2, 0) + 1) * T * P * 4] for b in range(B)]
+        x_c = [xc_t[min(b, 2)][:, max(b - 2, 0) * T * P:(max(b - 2, 0) + 1) * T * P] for b in range(B)]
+        x_s = [xs_t[min(b, 2)][:, max(b - 2, 0) * T * P:(max(b - 2, 0) + 1) * T * P] for b in range(B)]
+        gg_t = keep.tile([P, B * COUT * 4], BF16, name="gg_t", align_bytes=64)
+        gc_t = keep.tile([P, B * COUT], U32, name="gc_t", align_bytes=64)
+        gs_t = keep.tile([P, B * COUT], U8, name="gs_t", align_bytes=64)
+        g_g = [gg_t[:, b * COUT * 4:(b + 1) * COUT * 4] for b in range(B)]
+        g_c = [gc_t[:, b * COUT:(b + 1) * COUT] for b in range(B)]
+        g_s = [gs_t[:, b * COUT:(b + 1) * COUT] for b in range(B)]
         g0 = [[keep.tile([P, 2, COUT], F32, name="g0_%d_%d" % (b, h)) for h in range(2)] for b in range(B)]
         o_sb = [[keep.tile([P, 2, COUT], F32, name="o_sb%d_%d" % (b, h)) for h in range(2)] for b in range(B)]
         s_perm = keep.tile([P, T, NODES], F32, name="s_perm")
@@ -90,7 +96,6 @@ def tile_modulatedgraphconv_pa_kernel(tc, x, W, M, adj, adj2, bias, out):
             nc.sync.dma_start(out=w_raw[w][:], in_=W[w].rearrange("(u q e) c -> q u (e c)", u=2, q=P, e=2))
 
         def small_loads():
-            nc.sync.dma_start(out=brow[0:1, :], in_=bias.rearrange("(o c) -> o c", o=1))
             with nc.allow_non_contiguous_dma(reason="the 512 diagonal elements, one piece each"):
                 nc.sync.dma_start(
                     out=diag1[:],
@@ -100,9 +105,9 @@ def tile_modulatedgraphconv_pa_kernel(tc, x, W, M, adj, adj2, bias, out):
                     in_=adj2.rearrange("a b -> (a b)")[0:NODES * NODES:NODES + 1].rearrange("(p t) -> p t", t=T))
 
         def consts():
+            nc.gpsimd.memset(brow[:], 0.0)
             make_identity(nc, ident_f[:])
             nc.gpsimd.memset(warm_in[:], 0.0)
-            nc.gpsimd.memset(brow[:], 0.0)
             nc.gpsimd.memset(ones_b[:], 1.0)
             make_identity(nc, ident_b[:])
             nc.gpsimd.tensor_scalar(out=offmask[:], in0=ident_f[:], scalar1=-1.0, scalar2=1.0,
@@ -170,8 +175,11 @@ def tile_modulatedgraphconv_pa_kernel(tc, x, W, M, adj, adj2, bias, out):
             nc.vector.tensor_tensor(out=gv[:, cc, :], in0=live["h1", b, ch][:].rearrange("p t c -> p c t"),
                                     in1=m_sb[:, :, cc].rearrange("p t c -> p c t"), op=ALU.mult)
 
-        def op_QG(b):
-            nc.vector.quantize_mx(out=g_c[b][:].bitcast(FP8X4), scales=g_s[b][:], in_=g_g[b][:])
+        def op_QY():
+            nc.vector.quantize_mx(out=xc_t[2][:].bitcast(FP8X4), scales=xs_t[2][:], in_=xg_t[2][:])
+
+        def op_QH():
+            nc.vector.quantize_mx(out=gc_t[:].bitcast(FP8X4), scales=gs_t[:], in_=gg_t[:])
 
         def op_H0(b, h):
             h0 = psum.tile([P, 2, COUT], F32, tag="h0" + str(h), name="h0_%d_%d" % (b, h))
@@ -247,20 +255,21 @@ def tile_modulatedgraphconv_pa_kernel(tc, x, W, M, adj, adj2, bias, out):
             ts = slice(2 * h, 2 * h + 2)
             nc.sync.dma_start(out=out[b].rearrange("(p t) c -> p t c", t=T)[:, ts, :], in_=o_sb[b][h][:])
 
-        ops = {"XT": op_XT, "XC": op_XC, "QX": op_QX, "H1": op_H1, "G1": op_G1, "QG": op_QG, "H0": op_H0,
+        ops = {"XT": op_XT, "XC": op_XC, "QX": op_QX, "H1": op_H1, "G1": op_G1, "QY": op_QY, "QH": op_QH, "H0": op_H0,
                "G0": op_G0, "E0": op_E0, "P0": op_P0, "BI": op_BI, "SM": op_SM, "SE": op_SE, "MK": op_MK,
                "TR": op_TR, "AS": op_AS, "QA": op_QA, "AG": op_AG, "FI": op_FI, "ST": op_ST, "QW": op_QW,
                "BM": op_BM, "BE": op_BE, "AD": op_AD, "AM": op_AM}
 
         consts()
+        nc.scalar.dma_start(out=brow[0:1, :], in_=bias.rearrange("(o c) -> o c", o=1))
         nc.scalar.activation(out=warm_out[:], in_=warm_in[:], func=ACT.Copy)
         load_x_half(0, 0)
         load_x_half(0, 1)
         load_w(1)
         load_w(0)
-        small_loads()
         load_x(1)
         nc.sync.dma_start(out=m_sb[:], in_=M.rearrange("(p t) c -> p t c", t=T))
+        small_loads()
         load_x(2)
         load_x(3)
         nc.sync.dma_start(out=adj_sb[:], in_=adj.rearrange("(p t) i -> p t i", t=T))

@@ -14,25 +14,15 @@ ALU = mybir.AluOpType
 ACT = mybir.ActivationFunctionType
 
 P = 128
+PACK = 4
 B = 4
 NODES = 512
 CIN = 512
 COUT = 256
-T = 4
-
-MANUAL = True
-ORDER = (
-    "XT00", "XT01", "XC00", "WC1V", "XC01", "QW1", "WC0S", "QX0", "XT10", "XT11", "AD", "QW0",
-    "AM", "XC10", "BM", "H100", "XC11", "H101", "H000", "G100", "BE", "H001", "XT20", "G101",
-    "XT21", "QX1", "XC20", "XT30", "G000", "XC21", "G001", "H110", "XT31", "BI00", "XC30", "G110",
-    "H111", "H010", "XC31", "SM0", "G111", "BI01", "SM1", "QY", "SE0", "H011", "SM2", "SE1",
-    "G010", "MK0", "SE2", "G011", "H120", "MK1", "H121", "BI10", "SM3", "G120", "H020", "G121",
-    "H021", "SE3", "H130", "G020", "MK2", "H131", "G021", "TR0", "MK3", "G130", "TR1", "BI11",
-    "G131", "TR2", "QH", "TR3", "BI20", "H030", "H031", "AS0", "AS1", "AS2", "BI21", "AS3",
-    "QA", "G030", "G031", "AG00", "AG01", "BI30", "AG10", "FI00", "AG11", "AG20", "FI01", "AG21",
-    "ST00", "AG30", "FI10", "BI31", "AG31", "ST01", "FI11", "ST10", "FI20", "ST11", "FI21", "ST20",
-    "FI30", "ST21", "FI31", "ST30", "ST31",
-)
+T = NODES // P
+HALVES = 2
+T_HALF = T // HALVES
+RUN = 4
 
 
 def tile_modulatedgraphconv_pa_kernel(tc, x, W, M, adj, adj2, bias, out):
@@ -41,242 +31,214 @@ def tile_modulatedgraphconv_pa_kernel(tc, x, W, M, adj, adj2, bias, out):
         const = ctx.enter_context(tc.tile_pool(name="const", bufs=1))
         keep = ctx.enter_context(tc.tile_pool(name="keep", bufs=1))
         psum = ctx.enter_context(tc.psum_pool(name="psum", bufs=1))
-        if MANUAL:
-            ctx.enter_context(tc.manual_schedule())
+        ctx.enter_context(tc.manual_schedule())
+
+        def bank(pair, i, shape, name):
+            return psum.tile(shape, F32, tag="%s%d" % (pair, i), name=name)
 
         ident_f = const.tile([P, P], F32, name="ident_f")
         ident_b = const.tile([P, P], BF16, name="ident_b")
         ones_b = const.tile([P, P], BF16, name="ones_b")
-        brow = const.tile([P, COUT], BF16, name="brow")
-        offmask = const.tile([P, P], F32, name="offmask")
+        off_diag = const.tile([P, P], F32, name="off_diag")
+        bias_row = const.tile([P, COUT], BF16, name="bias_row")
         warm_in = const.tile([P, 1], F32, name="warm_in")
         warm_out = const.tile([P, 1], F32, name="warm_out")
 
-        w_raw = [keep.tile([P, 2, 512], BF16, name="w_raw%d" % w) for w in range(2)]
+        nc.gpsimd.memset(bias_row[:], 0.0)
+        make_identity(nc, ident_f[:])
+        nc.gpsimd.memset(warm_in[:], 0.0)
+        nc.gpsimd.memset(ones_b[:], 1.0)
+        make_identity(nc, ident_b[:])
+        nc.gpsimd.tensor_scalar(out=off_diag[:], in0=ident_f[:], scalar1=-1.0, scalar2=1.0,
+                                op0=ALU.mult, op1=ALU.add)
+
         x_sb = [keep.tile([P, T * CIN], BF16, name="x_sb%d" % b) for b in range(B)]
+        w_sb = [keep.tile([P, 2, 2 * COUT], BF16, name="w_sb%d" % w) for w in range(2)]
         m_sb = keep.tile([P, T, COUT], BF16, name="m_sb")
         adj_sb = keep.tile([P, T, NODES], BF16, name="adj_sb")
         adj2_sb = keep.tile([P, T, NODES], BF16, name="adj2_sb")
-        diag1 = keep.tile([P, T], BF16, name="diag1")
-        diag2 = keep.tile([P, T], BF16, name="diag2")
-        w_g = [keep.tile([P, 4 * COUT], BF16, name="w_g%d" % w, align_bytes=64) for w in range(2)]
-        w_c = [keep.tile([P, COUT], U32, name="w_c%d" % w, align_bytes=64) for w in range(2)]
-        w_s = [keep.tile([P, COUT], U8, name="w_s%d" % w, align_bytes=64) for w in range(2)]
-        bias2 = keep.tile([P, 2, COUT], F32, name="bias2")
-        a_self = keep.tile([P, T], F32, name="a_self")
-        a_m = keep.tile([P, T, COUT], F32, name="a_m")
-        xg_t = [keep.tile([P, n * T * P * 4], BF16, name="xg_t%d" % i, align_bytes=64) for i, n in enumerate((1, 1, 2))]
-        xc_t = [keep.tile([P, n * T * P], U32, name="xc_t%d" % i, align_bytes=64) for i, n in enumerate((1, 1, 2))]
-        xs_t = [keep.tile([P, n * T * P], U8, name="xs_t%d" % i, align_bytes=64) for i, n in enumerate((1, 1, 2))]
-        x_g = [xg_t[min(b, 2)][:, max(b - 2, 0) * T * P * 4:(max(b - 2, 0) + 1) * T * P * 4] for b in range(B)]
-        x_c = [xc_t[min(b, 2)][:, max(b - 2, 0) * T * P:(max(b - 2, 0) + 1) * T * P] for b in range(B)]
-        x_s = [xs_t[min(b, 2)][:, max(b - 2, 0) * T * P:(max(b - 2, 0) + 1) * T * P] for b in range(B)]
-        gg_t = keep.tile([P, B * COUT * 4], BF16, name="gg_t", align_bytes=64)
-        gc_t = keep.tile([P, B * COUT], U32, name="gc_t", align_bytes=64)
-        gs_t = keep.tile([P, B * COUT], U8, name="gs_t", align_bytes=64)
-        g_g = [gg_t[:, b * COUT * 4:(b + 1) * COUT * 4] for b in range(B)]
-        g_c = [gc_t[:, b * COUT:(b + 1) * COUT] for b in range(B)]
-        g_s = [gs_t[:, b * COUT:(b + 1) * COUT] for b in range(B)]
-        g0 = [[keep.tile([P, 2, COUT], F32, name="g0_%d_%d" % (b, h)) for h in range(2)] for b in range(B)]
-        o_sb = [[keep.tile([P, 2, COUT], F32, name="o_sb%d_%d" % (b, h)) for h in range(2)] for b in range(B)]
-        s_perm = keep.tile([P, T, NODES], F32, name="s_perm")
-        a_g = keep.tile([P, NODES * 4], BF16, name="a_g", align_bytes=64)
-        a_c = keep.tile([P, NODES], U32, name="a_c", align_bytes=64)
-        a_s = keep.tile([P, NODES], U8, name="a_s", align_bytes=64)
-        live = {}
+        diag_sb = [keep.tile([P, T], BF16, name="diag_sb%d" % i) for i in range(2)]
 
-        def load_x_half(b, h):
-            nc.sync.dma_start(out=x_sb[b][:, 2 * h * CIN:(2 * h + 2) * CIN].rearrange("p (t k) -> p t k", t=2),
-                              in_=x[b].rearrange("(p t) k -> p t k", t=T)[:, 2 * h:2 * h + 2, :])
-
-        def load_x(b):
-            nc.sync.dma_start(out=x_sb[b][:], in_=x[b].rearrange("(p t) k -> p (t k)", t=T))
-
-        def load_w(w):
-            nc.sync.dma_start(out=w_raw[w][:], in_=W[w].rearrange("(u q e) c -> q u (e c)", u=2, q=P, e=2))
-
-        def small_loads():
-            with nc.allow_non_contiguous_dma(reason="the 512 diagonal elements, one piece each"):
-                nc.sync.dma_start(
-                    out=diag1[:],
-                    in_=adj.rearrange("a b -> (a b)")[0:NODES * NODES:NODES + 1].rearrange("(p t) -> p t", t=T))
-                nc.sync.dma_start(
-                    out=diag2[:],
-                    in_=adj2.rearrange("a b -> (a b)")[0:NODES * NODES:NODES + 1].rearrange("(p t) -> p t", t=T))
-
-        def consts():
-            nc.gpsimd.memset(brow[:], 0.0)
-            make_identity(nc, ident_f[:])
-            nc.gpsimd.memset(warm_in[:], 0.0)
-            nc.gpsimd.memset(ones_b[:], 1.0)
-            make_identity(nc, ident_b[:])
-            nc.gpsimd.tensor_scalar(out=offmask[:], in0=ident_f[:], scalar1=-1.0, scalar2=1.0,
-                                    op0=ALU.mult, op1=ALU.add)
-
-        def op_WC(w, eng):
-            dst = w_g[w][:].rearrange("p (c i s) -> p c s i", i=4, s=4)
-            src = w_raw[w][:].rearrange("p u (e c i) -> p c (u e) i", e=2, i=4)
-            if eng == "V":
-                nc.vector.tensor_copy(out=dst, in_=src)
-            else:
-                nc.scalar.copy(out=dst, in_=src)
-
-        def op_QW(w):
-            nc.vector.quantize_mx(out=w_c[w][:].bitcast(FP8X4), scales=w_s[w][:], in_=w_g[w][:])
-
-        def op_BM():
-            bias_ps = psum.tile([P, COUT], F32, tag="aa0", name="bias_ps")
-            nc.tensor.matmul(out=bias_ps[:], lhsT=ones_b[:], rhs=brow[:], start=True, stop=True)
-            live["bias"] = bias_ps
-
-        def op_BE():
-            for r in range(2):
-                nc.scalar.copy(out=bias2[:, r, :], in_=live["bias"][:])
-
-        def op_AD():
-            nc.gpsimd.tensor_tensor(out=a_self[:], in0=diag1[:], in1=diag2[:], op=ALU.add)
-
-        def op_AM():
-            for t in range(T):
-                nc.gpsimd.tensor_scalar(out=a_m[:, t, :], in0=m_sb[:, t, :], scalar1=a_self[:, t:t + 1],
-                                        scalar2=0.0, op0=ALU.mult, op1=ALU.add)
-
-        def op_XT(b, h):
-            xw = x_sb[b][:, 2 * h * CIN:(2 * h + 2) * CIN].bitcast(F32)
-            xt = psum.tile([P, 2, 2, P], F32, tag=("aa" if b == 3 else "xt") + str(h), name="xt_%d_%d" % (b, h))
-            for tt in range(2):
-                for u in range(2):
-                    c0 = tt * 256 + u * P
-                    nc.tensor.transpose(xt[:, tt, u, :], xw[:, c0:c0 + P], ident_f[:])
-            live["xt", b, h] = xt
-
-        def op_XC(b, h):
-            gw = x_g[b][:].bitcast(F32).rearrange("p (t n u) -> p t n u", t=T, u=2)
-            nc.scalar.copy(out=gw[:, 2 * h:2 * h + 2, :, :],
-                           in_=live["xt", b, h][:].rearrange("p t u n -> p t n u"))
-
-        def op_QX(b):
-            nc.vector.quantize_mx(out=x_c[b][:].bitcast(FP8X4), scales=x_s[b][:], in_=x_g[b][:])
-
-        def op_H1(b, ch):
-            h1 = psum.tile([P, T, P], F32, tag="h1" + str(ch), name="h1_%d_%d" % (b, ch))
-            wc = slice(ch * P, (ch + 1) * P)
-            for t in range(T):
-                nodes = slice(t * P, (t + 1) * P)
-                nc.tensor.matmul_mx(out=h1[:, t, :],
-                                    lhsT=x_c[b][:, nodes].bitcast(FP8X4), lhsT_scale=x_s[b][:, nodes],
-                                    rhs=w_c[1][:, wc].bitcast(FP8X4), rhs_scale=w_s[1][:, wc],
-                                    start=True, stop=True)
-            live["h1", b, ch] = h1
-
-        def op_G1(b, ch):
-            gv = g_g[b][:].rearrange("p (c t) -> p c t", t=T)
-            cc = slice(ch * P, (ch + 1) * P)
-            nc.vector.tensor_tensor(out=gv[:, cc, :], in0=live["h1", b, ch][:].rearrange("p t c -> p c t"),
-                                    in1=m_sb[:, :, cc].rearrange("p t c -> p c t"), op=ALU.mult)
-
-        def op_QY():
-            nc.vector.quantize_mx(out=xc_t[2][:].bitcast(FP8X4), scales=xs_t[2][:], in_=xg_t[2][:])
-
-        def op_QH():
-            nc.vector.quantize_mx(out=gc_t[:].bitcast(FP8X4), scales=gs_t[:], in_=gg_t[:])
-
-        def op_H0(b, h):
-            h0 = psum.tile([P, 2, COUT], F32, tag="h0" + str(h), name="h0_%d_%d" % (b, h))
-            for tt in range(2):
-                nodes = slice((2 * h + tt) * P, (2 * h + tt + 1) * P)
-                nc.tensor.matmul_mx(out=h0[:, tt, :],
-                                    lhsT=x_c[b][:, nodes].bitcast(FP8X4), lhsT_scale=x_s[b][:, nodes],
-                                    rhs=w_c[0][:].bitcast(FP8X4), rhs_scale=w_s[0][:],
-                                    start=True, stop=True)
-            live["h0", b, h] = h0
-
-        def op_G0(b, h):
-            ts = slice(2 * h, 2 * h + 2)
-            nc.vector.tensor_tensor(out=g0[b][h][:], in0=live["h0", b, h][:], in1=a_m[:, ts, :], op=ALU.mult)
-
-        def op_E0(b, h):
-            ts = slice(2 * h, 2 * h + 2)
-            nc.scalar.copy(out=g0[b][h][:], in_=live["h0", b, h][:])
-
-        def op_P0(b, h):
-            ts = slice(2 * h, 2 * h + 2)
-            nc.gpsimd.tensor_tensor(out=g0[b][h][:], in0=g0[b][h][:], in1=a_m[:, ts, :], op=ALU.mult)
-
-        def op_BI(b, h):
-            ts = slice(2 * h, 2 * h + 2)
-            nc.gpsimd.tensor_tensor(out=g0[b][h][:], in0=g0[b][h][:], in1=bias2[:], op=ALU.add)
-
-        def op_SM(t):
-            s_ps = psum.tile([P, NODES], F32, tag=("xt" if t < 2 else "aa") + str(t % 2), name="s_ps%d" % t)
-            nc.tensor.matmul(out=s_ps[:], lhsT=ident_b[:], rhs=adj_sb[:, t, :], start=True, stop=False)
-            nc.tensor.matmul(out=s_ps[:], lhsT=ident_b[:], rhs=adj2_sb[:, t, :], start=False, stop=True)
-            live["s", t] = s_ps
-
-        def op_SE(t):
-            nc.scalar.activation(out=s_perm[:, t, :].rearrange("p (s c) -> p s c", s=T),
-                                 in_=live["s", t][:].rearrange("p (c s) -> p s c", s=T),
-                                 func=ACT.Copy, scale=0.5)
-
-        def op_MK(t):
-            blk = s_perm[:, t, t * P:(t + 1) * P]
-            nc.gpsimd.tensor_tensor(out=blk, in0=blk, in1=offmask[:], op=ALU.mult)
-
-        def op_TR(tp):
-            tr = psum.tile([P, T, P], F32, tag=("xt" if tp < 2 else "aa") + str(tp % 2), name="tr%d" % tp)
-            for t in range(T):
-                nc.tensor.transpose(tr[:, t, :], s_perm[:, tp, t * P:(t + 1) * P], ident_f[:])
-            live["tr", tp] = tr
-
-        def op_AS(tp):
-            av = a_g[:].rearrange("p (c t) -> p c t", t=T)
-            cc = slice(tp * P, (tp + 1) * P)
-            nc.vector.tensor_tensor(out=av[:, cc, :], in0=live["tr", tp][:].rearrange("p t c -> p c t"),
-                                    in1=s_perm[:, :, cc].rearrange("p t c -> p c t"), op=ALU.add)
-
-        def op_QA():
-            nc.vector.quantize_mx(out=a_c[:].bitcast(FP8X4), scales=a_s[:], in_=a_g[:])
-
-        def op_AG(b, h):
-            agg = psum.tile([P, 2, COUT], F32, tag=("xt", "aa", "h1", "h0")[b] + str(h), name="agg_%d_%d" % (b, h))
-            for tt in range(2):
-                rows = slice((2 * h + tt) * P, (2 * h + tt + 1) * P)
-                nc.tensor.matmul_mx(out=agg[:, tt, :],
-                                    lhsT=a_c[:, rows].bitcast(FP8X4), lhsT_scale=a_s[:, rows],
-                                    rhs=g_c[b][:].bitcast(FP8X4), rhs_scale=g_s[b][:],
-                                    start=True, stop=True)
-            live["agg", b, h] = agg
-
-        def op_FI(b, h):
-            ts = slice(2 * h, 2 * h + 2)
-            nc.vector.tensor_tensor(out=o_sb[b][h][:], in0=live["agg", b, h][:], in1=g0[b][h][:], op=ALU.add)
-
-        def op_ST(b, h):
-            ts = slice(2 * h, 2 * h + 2)
-            nc.sync.dma_start(out=out[b].rearrange("(p t) c -> p t c", t=T)[:, ts, :], in_=o_sb[b][h][:])
-
-        ops = {"XT": op_XT, "XC": op_XC, "QX": op_QX, "H1": op_H1, "G1": op_G1, "QY": op_QY, "QH": op_QH, "H0": op_H0,
-               "G0": op_G0, "E0": op_E0, "P0": op_P0, "BI": op_BI, "SM": op_SM, "SE": op_SE, "MK": op_MK,
-               "TR": op_TR, "AS": op_AS, "QA": op_QA, "AG": op_AG, "FI": op_FI, "ST": op_ST, "QW": op_QW,
-               "BM": op_BM, "BE": op_BE, "AD": op_AD, "AM": op_AM}
-
-        consts()
-        nc.scalar.dma_start(out=brow[0:1, :], in_=bias.rearrange("(o c) -> o c", o=1))
+        nc.scalar.dma_start(out=bias_row[0:1, :], in_=bias.rearrange("(o c) -> o c", o=1))
         nc.scalar.activation(out=warm_out[:], in_=warm_in[:], func=ACT.Copy)
-        load_x_half(0, 0)
-        load_x_half(0, 1)
-        load_w(1)
-        load_w(0)
-        load_x(1)
+
+        for h in range(HALVES):
+            nc.sync.dma_start(
+                out=x_sb[0][:, h * T_HALF * CIN:(h + 1) * T_HALF * CIN].rearrange("p (t k) -> p t k", t=T_HALF),
+                in_=x[0].rearrange("(p t) k -> p t k", t=T)[:, h * T_HALF:(h + 1) * T_HALF, :])
+        for w in (1, 0):
+            nc.sync.dma_start(out=w_sb[w][:], in_=W[w].rearrange("(u q e) c -> q u (e c)", u=2, q=P, e=2))
+        nc.sync.dma_start(out=x_sb[1][:], in_=x[1].rearrange("(p t) k -> p (t k)", t=T))
         nc.sync.dma_start(out=m_sb[:], in_=M.rearrange("(p t) c -> p t c", t=T))
-        small_loads()
-        load_x(2)
-        load_x(3)
+        with nc.allow_non_contiguous_dma(reason="the 512 diagonal elements of a matrix, one piece each"):
+            for i, matrix in enumerate((adj, adj2)):
+                nc.sync.dma_start(
+                    out=diag_sb[i][:],
+                    in_=matrix.rearrange("a b -> (a b)")[0:NODES * NODES:NODES + 1].rearrange("(p t) -> p t", t=T))
+        for b in (2, 3):
+            nc.sync.dma_start(out=x_sb[b][:], in_=x[b].rearrange("(p t) k -> p (t k)", t=T))
         nc.sync.dma_start(out=adj_sb[:], in_=adj.rearrange("(p t) i -> p t i", t=T))
         nc.sync.dma_start(out=adj2_sb[:], in_=adj2.rearrange("(p t) i -> p t i", t=T))
-        for word in ORDER:
-            kind = word[0:2]
-            if kind == "WC":
-                op_WC(int(word[2]), word[3])
-            else:
-                ops[kind](*[int(d) for d in word[2:]])
+
+        XW = T * P
+        w_grouped = [keep.tile([P, COUT * PACK], BF16, name="w_grouped%d" % w, align_bytes=64) for w in range(2)]
+        w_codes = [keep.tile([P, COUT], U32, name="w_codes%d" % w, align_bytes=64) for w in range(2)]
+        w_scales = [keep.tile([P, COUT], U8, name="w_scales%d" % w, align_bytes=64) for w in range(2)]
+        x_batches = ((0,), (1,), (2, 3))
+        x_grouped = [keep.tile([P, len(bs) * XW * PACK], BF16, name="x_grouped%d" % i, align_bytes=64)
+                     for i, bs in enumerate(x_batches)]
+        x_codes = [keep.tile([P, len(bs) * XW], U32, name="x_codes%d" % i, align_bytes=64)
+                   for i, bs in enumerate(x_batches)]
+        x_scales = [keep.tile([P, len(bs) * XW], U8, name="x_scales%d" % i, align_bytes=64)
+                    for i, bs in enumerate(x_batches)]
+        g_grouped = keep.tile([P, B * COUT * PACK], BF16, name="g_grouped", align_bytes=64)
+        g_codes = keep.tile([P, B * COUT], U32, name="g_codes", align_bytes=64)
+        g_scales = keep.tile([P, B * COUT], U8, name="g_scales", align_bytes=64)
+        a_grouped = keep.tile([P, NODES * PACK], BF16, name="a_grouped", align_bytes=64)
+        a_codes = keep.tile([P, NODES], U32, name="a_codes", align_bytes=64)
+        a_scales = keep.tile([P, NODES], U8, name="a_scales", align_bytes=64)
+
+        def x_part(tiles, b, width):
+            i = min(b, 2)
+            first = (b - x_batches[i][0]) * width
+            return tiles[i][:, first:first + width]
+
+        def quantise(codes, scales, grouped):
+            nc.vector.quantize_mx(out=codes.bitcast(FP8X4), scales=scales, in_=grouped)
+
+        def mx(acc, lhs_codes, lhs_scales, rhs_codes, rhs_scales):
+            nc.tensor.matmul_mx(out=acc, lhsT=lhs_codes.bitcast(FP8X4), lhsT_scale=lhs_scales,
+                                rhs=rhs_codes.bitcast(FP8X4), rhs_scale=rhs_scales, start=True, stop=True)
+
+        bias_all = keep.tile([P, T_HALF, COUT], F32, name="bias_all")
+        a_self = keep.tile([P, T], F32, name="a_self")
+        a_self_m = keep.tile([P, T, COUT], F32, name="a_self_m")
+        a_half = keep.tile([P, T, NODES], F32, name="a_half")
+        self_term = [[keep.tile([P, T_HALF, COUT], F32, name="self_term%d_%d" % (b, h)) for h in range(HALVES)]
+                     for b in range(B)]
+        result = [[keep.tile([P, T_HALF, COUT], F32, name="result%d_%d" % (b, h)) for h in range(HALVES)]
+                  for b in range(B)]
+
+        def transpose_x(b):
+            words = x_sb[b][:].bitcast(F32).rearrange("p (t u q) -> p t u q", t=T, u=2)
+            grouped = x_part(x_grouped, b, XW * PACK).bitcast(F32).rearrange("q (t n u) -> q t n u", t=T, u=2)
+            for h in range(HALVES):
+                x_t = bank("sp" if b == 3 else "xt", h, [P, T_HALF, 2, P], "x_t%d_%d" % (b, h))
+                for tt in range(T_HALF):
+                    for u in range(2):
+                        nc.tensor.transpose(x_t[:, tt, u, :], words[:, h * T_HALF + tt, u, :], ident_f[:])
+                nc.scalar.copy(out=grouped[:, h * T_HALF:(h + 1) * T_HALF, :, :],
+                               in_=x_t[:].rearrange("q t u n -> q t n u"))
+
+        def regroup_w(w, copy):
+            copy(out=w_grouped[w][:].rearrange("q (c i s) -> q c s i", i=RUN, s=PACK),
+                 in_=w_sb[w][:].rearrange("q u (e c i) -> q c (u e) i", e=2, i=RUN))
+
+        def spread_bias():
+            acc = bank("sp", 0, [P, COUT], "bias_acc")
+            nc.tensor.matmul(out=acc[:], lhsT=ones_b[:], rhs=bias_row[:], start=True, stop=True)
+            for r in range(T_HALF):
+                nc.scalar.copy(out=bias_all[:, r, :], in_=acc[:])
+
+        def self_gain():
+            nc.gpsimd.tensor_tensor(out=a_self[:], in0=diag_sb[0][:], in1=diag_sb[1][:], op=ALU.add)
+            for t in range(T):
+                nc.gpsimd.tensor_scalar(out=a_self_m[:, t, :], in0=m_sb[:, t, :], scalar1=a_self[:, t:t + 1],
+                                        scalar2=0.0, op0=ALU.mult, op1=ALU.add)
+
+        h1_acc = {}
+        h0_acc = {}
+
+        def project(b):
+            codes = x_part(x_codes, b, XW)
+            scales = x_part(x_scales, b, XW)
+            for h in range(HALVES):
+                h1_acc[b, h] = bank("h1", h, [P, T, P], "h1_acc%d_%d" % (b, h))
+                for t in range(T):
+                    mx(h1_acc[b, h][:, t, :], codes[:, t * P:(t + 1) * P], scales[:, t * P:(t + 1) * P],
+                       w_codes[1][:, h * P:(h + 1) * P], w_scales[1][:, h * P:(h + 1) * P])
+            for h in range(HALVES):
+                h0_acc[b, h] = bank("h0", h, [P, T_HALF, COUT], "h0_acc%d_%d" % (b, h))
+                for tt in range(T_HALF):
+                    t = h * T_HALF + tt
+                    mx(h0_acc[b, h][:, tt, :], codes[:, t * P:(t + 1) * P], scales[:, t * P:(t + 1) * P],
+                       w_codes[0][:], w_scales[0][:])
+
+        def modulate_h1(b):
+            grouped = g_grouped[:, b * COUT * PACK:(b + 1) * COUT * PACK].rearrange("p (c t) -> p c t", t=T)
+            for h in range(HALVES):
+                nc.vector.tensor_tensor(out=grouped[:, h * P:(h + 1) * P, :],
+                                        in0=h1_acc[b, h][:].rearrange("p t c -> p c t"),
+                                        in1=m_sb[:, :, h * P:(h + 1) * P].rearrange("p t c -> p c t"), op=ALU.mult)
+
+        def add_self_term(b):
+            for h in range(HALVES):
+                nc.vector.tensor_tensor(out=self_term[b][h][:], in0=h0_acc[b, h][:],
+                                        in1=a_self_m[:, h * T_HALF:(h + 1) * T_HALF, :], op=ALU.mult)
+                nc.gpsimd.tensor_tensor(out=self_term[b][h][:], in0=self_term[b][h][:], in1=bias_all[:],
+                                        op=ALU.add)
+
+        def a_pair(t):
+            return "xt" if t < HALVES else "sp"
+
+        def half_sum_rows(t):
+            acc = bank(a_pair(t), t % HALVES, [P, NODES], "a_acc%d" % t)
+            nc.tensor.matmul(out=acc[:], lhsT=ident_b[:], rhs=adj_sb[:, t, :], start=True, stop=False)
+            nc.tensor.matmul(out=acc[:], lhsT=ident_b[:], rhs=adj2_sb[:, t, :], start=False, stop=True)
+            nc.scalar.activation(out=a_half[:, t, :].rearrange("p (s c) -> p s c", s=T),
+                                 in_=acc[:].rearrange("p (c s) -> p s c", s=T), func=ACT.Copy, scale=0.5)
+            block = a_half[:, t, t * P:(t + 1) * P]
+            nc.gpsimd.tensor_tensor(out=block, in0=block, in1=off_diag[:], op=ALU.mult)
+
+        def symmetrise():
+            grouped = a_grouped[:].rearrange("p (i t) -> p i t", t=T)
+            flipped = {}
+            for s in range(T):
+                flipped[s] = bank(a_pair(s), s % HALVES, [P, T, P], "a_flipped%d" % s)
+                for t in range(T):
+                    nc.tensor.transpose(flipped[s][:, t, :], a_half[:, s, t * P:(t + 1) * P], ident_f[:])
+            for s in range(T):
+                nc.vector.tensor_tensor(out=grouped[:, s * P:(s + 1) * P, :],
+                                        in0=flipped[s][:].rearrange("p t c -> p c t"),
+                                        in1=a_half[:, :, s * P:(s + 1) * P].rearrange("p t c -> p c t"), op=ALU.add)
+
+        def aggregate(b):
+            rows = out[b].rearrange("(p t) c -> p t c", t=T)
+            acc = {}
+            for h in range(HALVES):
+                acc[h] = bank(("xt", "sp", "h1", "h0")[b], h, [P, T_HALF, COUT], "agg_acc%d_%d" % (b, h))
+                for tt in range(T_HALF):
+                    s = h * T_HALF + tt
+                    mx(acc[h][:, tt, :], a_codes[:, s * P:(s + 1) * P], a_scales[:, s * P:(s + 1) * P],
+                       g_codes[:, b * COUT:(b + 1) * COUT], g_scales[:, b * COUT:(b + 1) * COUT])
+            for h in range(HALVES):
+                nc.vector.tensor_tensor(out=result[b][h][:], in0=acc[h][:], in1=self_term[b][h][:], op=ALU.add)
+                nc.sync.dma_start(out=rows[:, h * T_HALF:(h + 1) * T_HALF, :], in_=result[b][h][:])
+
+        transpose_x(0)
+        regroup_w(1, nc.vector.tensor_copy)
+        regroup_w(0, nc.scalar.copy)
+        quantise(w_codes[1][:], w_scales[1][:], w_grouped[1][:])
+        quantise(x_codes[0][:], x_scales[0][:], x_grouped[0][:])
+        quantise(w_codes[0][:], w_scales[0][:], w_grouped[0][:])
+        spread_bias()
+        transpose_x(1)
+        self_gain()
+        for b in range(B):
+            project(b)
+            if b == 0:
+                transpose_x(2)
+                transpose_x(3)
+            if b == 1:
+                for t in range(T):
+                    half_sum_rows(t)
+            modulate_h1(b)
+            if b < 2:
+                quantise(x_codes[b + 1][:], x_scales[b + 1][:], x_grouped[b + 1][:])
+            if b == B - 1:
+                quantise(g_codes[:], g_scales[:], g_grouped[:])
+                symmetrise()
+                quantise(a_codes[:], a_scales[:], a_grouped[:])
+            add_self_term(b)
+        for b in range(B):
+            aggregate(b)

@@ -23,6 +23,7 @@ T = NODES // P
 HALVES = 2
 T_HALF = T // HALVES
 RUN = 4
+SELF_TERM_OFF_VECTOR = (2,)
 
 
 def tile_modulatedgraphconv_pa_kernel(tc, x, W, M, adj, adj2, bias, out):
@@ -173,8 +174,12 @@ def tile_modulatedgraphconv_pa_kernel(tc, x, W, M, adj, adj2, bias, out):
 
         def add_self_term(b):
             for h in range(HALVES):
-                nc.vector.tensor_tensor(out=self_term[b][h][:], in0=h0_acc[b, h][:],
-                                        in1=a_self_m[:, h * T_HALF:(h + 1) * T_HALF, :], op=ALU.mult)
+                gain = a_self_m[:, h * T_HALF:(h + 1) * T_HALF, :]
+                if b in SELF_TERM_OFF_VECTOR:
+                    nc.scalar.copy(out=self_term[b][h][:], in_=h0_acc[b, h][:])
+                    nc.gpsimd.tensor_tensor(out=self_term[b][h][:], in0=self_term[b][h][:], in1=gain, op=ALU.mult)
+                else:
+                    nc.vector.tensor_tensor(out=self_term[b][h][:], in0=h0_acc[b, h][:], in1=gain, op=ALU.mult)
                 nc.gpsimd.tensor_tensor(out=self_term[b][h][:], in0=self_term[b][h][:], in1=bias_all[:],
                                         op=ALU.add)
 

@@ -23,7 +23,7 @@ T = NODES // P
 HALVES = 2
 T_HALF = T // HALVES
 RUN = 4
-SELF_TERM_OFF_VECTOR = (2,)
+SELF_TERM_OFF_VECTOR = ((1, 1), (2, 1))
 
 
 def tile_modulatedgraphconv_pa_kernel(tc, x, W, M, adj, adj2, bias, out):
@@ -67,9 +67,12 @@ def tile_modulatedgraphconv_pa_kernel(tc, x, W, M, adj, adj2, bias, out):
             nc.sync.dma_start(
                 out=x_sb[0][:, h * T_HALF * CIN:(h + 1) * T_HALF * CIN].rearrange("p (t k) -> p t k", t=T_HALF),
                 in_=x[0].rearrange("(p t) k -> p t k", t=T)[:, h * T_HALF:(h + 1) * T_HALF, :])
-        for w in (1, 0):
+        def load_w(w):
             nc.sync.dma_start(out=w_sb[w][:], in_=W[w].rearrange("(u q e) c -> q u (e c)", u=2, q=P, e=2))
+
+        load_w(1)
         nc.sync.dma_start(out=x_sb[1][:], in_=x[1].rearrange("(p t) k -> p (t k)", t=T))
+        load_w(0)
         nc.sync.dma_start(out=m_sb[:], in_=M.rearrange("(p t) c -> p t c", t=T))
         with nc.allow_non_contiguous_dma(reason="the 512 diagonal elements of a matrix, one piece each"):
             for i, matrix in enumerate((adj, adj2)):
@@ -85,7 +88,7 @@ def tile_modulatedgraphconv_pa_kernel(tc, x, W, M, adj, adj2, bias, out):
         w_grouped = [keep.tile([P, COUT * PACK], BF16, name="w_grouped%d" % w, align_bytes=64) for w in range(2)]
         w_codes = [keep.tile([P, COUT], U32, name="w_codes%d" % w, align_bytes=64) for w in range(2)]
         w_scales = [keep.tile([P, COUT], U8, name="w_scales%d" % w, align_bytes=64) for w in range(2)]
-        x_batches = ((0,), (1,), (2, 3))
+        x_batches = ((0,), (1,), (2,), (3,))
         x_grouped = [keep.tile([P, len(bs) * XW * PACK], BF16, name="x_grouped%d" % i, align_bytes=64)
                      for i, bs in enumerate(x_batches)]
         x_codes = [keep.tile([P, len(bs) * XW], U32, name="x_codes%d" % i, align_bytes=64)
@@ -100,9 +103,7 @@ def tile_modulatedgraphconv_pa_kernel(tc, x, W, M, adj, adj2, bias, out):
         a_scales = keep.tile([P, NODES], U8, name="a_scales", align_bytes=64)
 
         def x_part(tiles, b, width):
-            i = min(b, 2)
-            first = (b - x_batches[i][0]) * width
-            return tiles[i][:, first:first + width]
+            return tiles[b][:, 0:width]
 
         def quantise(codes, scales, grouped):
             nc.vector.quantize_mx(out=codes.bitcast(FP8X4), scales=scales, in_=grouped)
@@ -150,7 +151,7 @@ def tile_modulatedgraphconv_pa_kernel(tc, x, W, M, adj, adj2, bias, out):
         h1_acc = {}
         h0_acc = {}
 
-        def project(b):
+        def project_h1(b):
             codes = x_part(x_codes, b, XW)
             scales = x_part(x_scales, b, XW)
             for h in range(HALVES):
@@ -158,6 +159,10 @@ def tile_modulatedgraphconv_pa_kernel(tc, x, W, M, adj, adj2, bias, out):
                 for t in range(T):
                     mx(h1_acc[b, h][:, t, :], codes[:, t * P:(t + 1) * P], scales[:, t * P:(t + 1) * P],
                        w_codes[1][:, h * P:(h + 1) * P], w_scales[1][:, h * P:(h + 1) * P])
+
+        def project_h0(b):
+            codes = x_part(x_codes, b, XW)
+            scales = x_part(x_scales, b, XW)
             for h in range(HALVES):
                 h0_acc[b, h] = bank("h0", h, [P, T_HALF, COUT], "h0_acc%d_%d" % (b, h))
                 for tt in range(T_HALF):
@@ -165,17 +170,21 @@ def tile_modulatedgraphconv_pa_kernel(tc, x, W, M, adj, adj2, bias, out):
                     mx(h0_acc[b, h][:, tt, :], codes[:, t * P:(t + 1) * P], scales[:, t * P:(t + 1) * P],
                        w_codes[0][:], w_scales[0][:])
 
-        def modulate_h1(b):
+        def modulate_h1(b, h):
             grouped = g_grouped[:, b * COUT * PACK:(b + 1) * COUT * PACK].rearrange("p (c t) -> p c t", t=T)
-            for h in range(HALVES):
-                nc.vector.tensor_tensor(out=grouped[:, h * P:(h + 1) * P, :],
-                                        in0=h1_acc[b, h][:].rearrange("p t c -> p c t"),
-                                        in1=m_sb[:, :, h * P:(h + 1) * P].rearrange("p t c -> p c t"), op=ALU.mult)
+            nc.vector.tensor_tensor(out=grouped[:, h * P:(h + 1) * P, :],
+                                    in0=h1_acc[b, h][:].rearrange("p t c -> p c t"),
+                                    in1=m_sb[:, :, h * P:(h + 1) * P].rearrange("p t c -> p c t"), op=ALU.mult)
+
+        def quantise_g(i):
+            w = 2 * COUT
+            quantise(g_codes[:, i * w:(i + 1) * w], g_scales[:, i * w:(i + 1) * w],
+                     g_grouped[:, i * w * PACK:(i + 1) * w * PACK])
 
         def add_self_term(b):
             for h in range(HALVES):
                 gain = a_self_m[:, h * T_HALF:(h + 1) * T_HALF, :]
-                if b in SELF_TERM_OFF_VECTOR:
+                if (b, h) in SELF_TERM_OFF_VECTOR:
                     nc.scalar.copy(out=self_term[b][h][:], in_=h0_acc[b, h][:])
                     nc.gpsimd.tensor_tensor(out=self_term[b][h][:], in0=self_term[b][h][:], in1=gain, op=ALU.mult)
                 else:
@@ -225,23 +234,28 @@ def tile_modulatedgraphconv_pa_kernel(tc, x, W, M, adj, adj2, bias, out):
         regroup_w(0, nc.scalar.copy)
         quantise(w_codes[1][:], w_scales[1][:], w_grouped[1][:])
         quantise(x_codes[0][:], x_scales[0][:], x_grouped[0][:])
-        quantise(w_codes[0][:], w_scales[0][:], w_grouped[0][:])
-        spread_bias()
         transpose_x(1)
+        spread_bias()
         self_gain()
         for b in range(B):
-            project(b)
+            project_h1(b)
+            if b == 1:
+                transpose_x(3)
+            modulate_h1(b, 0)
+            if b == 0:
+                quantise(w_codes[0][:], w_scales[0][:], w_grouped[0][:])
+            modulate_h1(b, 1)
+            project_h0(b)
             if b == 0:
                 transpose_x(2)
-                transpose_x(3)
             if b == 1:
                 for t in range(T):
                     half_sum_rows(t)
-            modulate_h1(b)
-            if b < 2:
+            if b < B - 1:
                 quantise(x_codes[b + 1][:], x_scales[b + 1][:], x_grouped[b + 1][:])
+            if b >= 2:
+                quantise_g(b - 2)
             if b == B - 1:
-                quantise(g_codes[:], g_scales[:], g_grouped[:])
                 symmetrise()
                 quantise(a_codes[:], a_scales[:], a_grouped[:])
             add_self_term(b)

@@ -23,7 +23,7 @@ T = NODES // P
 HALVES = 2
 T_HALF = T // HALVES
 RUN = 4
-SELF_TERM_OFF_VECTOR = ((1, 1), (2, 1))
+SELF_TERM_OFF_VECTOR = ((3, 0), (3, 1))
 
 
 def tile_modulatedgraphconv_pa_kernel(tc, x, W, M, adj, adj2, bias, out):
@@ -248,7 +248,7 @@ def tile_modulatedgraphconv_pa_kernel(tc, x, W, M, adj, adj2, bias, out):
             project_h0(b)
             if b == 0:
                 transpose_x(2)
-            if b == 1:
+            if b == 2:
                 for t in range(T):
                     half_sum_rows(t)
             if b < B - 1:

@@ -23,7 +23,7 @@ T = NODES // P
 HALVES = 2
 T_HALF = T // HALVES
 RUN = 4
-SELF_TERM_OFF_VECTOR = ((3, 0), (3, 1))
+ROWS_ADDED_BY_GPSIMD = (2, 3)
 
 
 def tile_modulatedgraphconv_pa_kernel(tc, x, W, M, adj, adj2, bias, out):
@@ -39,8 +39,8 @@ def tile_modulatedgraphconv_pa_kernel(tc, x, W, M, adj, adj2, bias, out):
 
         ident_f = const.tile([P, P], F32, name="ident_f")
         ident_b = const.tile([P, P], BF16, name="ident_b")
+        ident_4 = const.tile([P, T, P], BF16, name="ident_4")
         ones_b = const.tile([P, P], BF16, name="ones_b")
-        off_diag = const.tile([P, P], F32, name="off_diag")
         bias_row = const.tile([P, COUT], BF16, name="bias_row")
         warm_in = const.tile([P, 1], F32, name="warm_in")
         warm_out = const.tile([P, 1], F32, name="warm_out")
@@ -50,18 +50,17 @@ def tile_modulatedgraphconv_pa_kernel(tc, x, W, M, adj, adj2, bias, out):
         nc.gpsimd.memset(warm_in[:], 0.0)
         nc.gpsimd.memset(ones_b[:], 1.0)
         make_identity(nc, ident_b[:])
-        nc.gpsimd.tensor_scalar(out=off_diag[:], in0=ident_f[:], scalar1=-1.0, scalar2=1.0,
-                                op0=ALU.mult, op1=ALU.add)
 
         x_sb = [keep.tile([P, T * CIN], BF16, name="x_sb%d" % b) for b in range(B)]
         w_sb = [keep.tile([P, 2, 2 * COUT], BF16, name="w_sb%d" % w) for w in range(2)]
         m_sb = keep.tile([P, T, COUT], BF16, name="m_sb")
-        adj_sb = keep.tile([P, T, NODES], BF16, name="adj_sb")
-        adj2_sb = keep.tile([P, T, NODES], BF16, name="adj2_sb")
-        diag_sb = [keep.tile([P, T], BF16, name="diag_sb%d" % i) for i in range(2)]
+        adj_flat = [keep.tile([P, T * (NODES + 1)], BF16, name="adj_flat%d" % m) for m in range(2)]
+        adj_sb, adj2_sb = [flat[:, 0:T * NODES].rearrange("p (t i) -> p t i", t=T) for flat in adj_flat]
 
         nc.scalar.dma_start(out=bias_row[0:1, :], in_=bias.rearrange("(o c) -> o c", o=1))
         nc.scalar.activation(out=warm_out[:], in_=warm_in[:], func=ACT.Copy)
+        for t in range(T):
+            nc.scalar.copy(out=ident_4[:, t, :], in_=ident_b[:])
 
         for h in range(HALVES):
             nc.sync.dma_start(
@@ -72,17 +71,12 @@ def tile_modulatedgraphconv_pa_kernel(tc, x, W, M, adj, adj2, bias, out):
 
         load_w(1)
         nc.sync.dma_start(out=x_sb[1][:], in_=x[1].rearrange("(p t) k -> p (t k)", t=T))
-        load_w(0)
         nc.sync.dma_start(out=m_sb[:], in_=M.rearrange("(p t) c -> p t c", t=T))
-        with nc.allow_non_contiguous_dma(reason="the 512 diagonal elements of a matrix, one piece each"):
-            for i, matrix in enumerate((adj, adj2)):
-                nc.sync.dma_start(
-                    out=diag_sb[i][:],
-                    in_=matrix.rearrange("a b -> (a b)")[0:NODES * NODES:NODES + 1].rearrange("(p t) -> p t", t=T))
-        for b in (2, 3):
-            nc.sync.dma_start(out=x_sb[b][:], in_=x[b].rearrange("(p t) k -> p (t k)", t=T))
-        nc.sync.dma_start(out=adj_sb[:], in_=adj.rearrange("(p t) i -> p t i", t=T))
-        nc.sync.dma_start(out=adj2_sb[:], in_=adj2.rearrange("(p t) i -> p t i", t=T))
+        load_w(0)
+        nc.sync.dma_start(out=x_sb[2][:], in_=x[2].rearrange("(p t) k -> p (t k)", t=T))
+        nc.sync.dma_start(out=adj_sb, in_=adj.rearrange("(p t) i -> p t i", t=T))
+        nc.sync.dma_start(out=adj2_sb, in_=adj2.rearrange("(p t) i -> p t i", t=T))
+        nc.sync.dma_start(out=x_sb[3][:], in_=x[3].rearrange("(p t) k -> p (t k)", t=T))
 
         XW = T * P
         w_grouped = [keep.tile([P, COUT * PACK], BF16, name="w_grouped%d" % w, align_bytes=64) for w in range(2)]
@@ -114,8 +108,12 @@ def tile_modulatedgraphconv_pa_kernel(tc, x, W, M, adj, adj2, bias, out):
 
         bias_all = keep.tile([P, T_HALF, COUT], F32, name="bias_all")
         a_self = keep.tile([P, T], F32, name="a_self")
+        a_self_neg = keep.tile([P, T], F32, name="a_self_neg")
+        minus_diag = [keep.tile([P, P], F32, name="minus_diag%d" % s) for s in range(T)]
         a_self_m = keep.tile([P, T, COUT], F32, name="a_self_m")
-        a_half = keep.tile([P, T, NODES], F32, name="a_half")
+        diagonals = [keep.tile([P, T, P], BF16, name="diagonals%d" % m) for m in range(2)]
+        rows_f = [[keep.tile([P, NODES], F32, name="rows_f%d_%d" % (s, m))
+                   for m in range(1 if s in ROWS_ADDED_BY_GPSIMD else 2)] for s in range(T)]
         self_term = [[keep.tile([P, T_HALF, COUT], F32, name="self_term%d_%d" % (b, h)) for h in range(HALVES)]
                      for b in range(B)]
         result = [[keep.tile([P, T_HALF, COUT], F32, name="result%d_%d" % (b, h)) for h in range(HALVES)]
@@ -125,7 +123,7 @@ def tile_modulatedgraphconv_pa_kernel(tc, x, W, M, adj, adj2, bias, out):
             words = x_sb[b][:].bitcast(F32).rearrange("p (t u q) -> p t u q", t=T, u=2)
             grouped = x_part(x_grouped, b, XW * PACK).bitcast(F32).rearrange("q (t n u) -> q t n u", t=T, u=2)
             for h in range(HALVES):
-                x_t = bank("sp" if b == 3 else "xt", h, [P, T_HALF, 2, P], "x_t%d_%d" % (b, h))
+                x_t = bank("xt", h, [P, T_HALF, 2, P], "x_t%d_%d" % (b, h))
                 for tt in range(T_HALF):
                     for u in range(2):
                         nc.tensor.transpose(x_t[:, tt, u, :], words[:, h * T_HALF + tt, u, :], ident_f[:])
@@ -142,13 +140,33 @@ def tile_modulatedgraphconv_pa_kernel(tc, x, W, M, adj, adj2, bias, out):
             for r in range(T_HALF):
                 nc.scalar.copy(out=bias_all[:, r, :], in_=acc[:])
 
-        def self_gain():
-            nc.gpsimd.tensor_tensor(out=a_self[:], in0=diag_sb[0][:], in1=diag_sb[1][:], op=ALU.add)
+        def sorted_columns(matrix, t):
+            return matrix[:, t, :].rearrange("p (c s) -> p s c", s=T)
+
+        def mask_diagonals():
+            for m in range(2):
+                blocks = adj_flat[m][:].rearrange("p (t r) -> p t r", t=T)[:, :, 0:NODES:T]
+                nc.gpsimd.tensor_tensor(out=diagonals[m][:], in0=blocks, in1=ident_4[:], op=ALU.mult)
+
+        def gather_diagonal():
+            acc = bank("h0", 0, [P, T], "diag_acc")
             for t in range(T):
-                nc.gpsimd.tensor_scalar(out=a_self_m[:, t, :], in0=m_sb[:, t, :], scalar1=a_self[:, t:t + 1],
-                                        scalar2=0.0, op0=ALU.mult, op1=ALU.add)
+                for m in range(2):
+                    nc.tensor.matmul(out=acc[:, t:t + 1], lhsT=diagonals[m][:, t, :], rhs=ones_b[:, 0:1],
+                                     start=m == 0, stop=m == 1)
+            nc.scalar.copy(out=a_self[:], in_=acc[:])
+
+        def self_gain():
+            for t in range(T):
+                nc.scalar.activation(out=a_self_m[:, t, :], in_=m_sb[:, t, :], func=ACT.Copy, scale=a_self[:, t:t + 1])
+
+        def negative_diagonals():
+            nc.scalar.activation(out=a_self_neg[:], in_=a_self[:], func=ACT.Copy, scale=-1.0)
+            for s in range(T):
+                nc.scalar.activation(out=minus_diag[s][:], in_=ident_f[:], func=ACT.Copy, scale=a_self_neg[:, s:s + 1])
 
         h1_acc = {}
+        agg_acc = {}
         h0_acc = {}
 
         def project_h1(b):
@@ -184,80 +202,108 @@ def tile_modulatedgraphconv_pa_kernel(tc, x, W, M, adj, adj2, bias, out):
         def add_self_term(b):
             for h in range(HALVES):
                 gain = a_self_m[:, h * T_HALF:(h + 1) * T_HALF, :]
-                if (b, h) in SELF_TERM_OFF_VECTOR:
-                    nc.scalar.copy(out=self_term[b][h][:], in_=h0_acc[b, h][:])
-                    nc.gpsimd.tensor_tensor(out=self_term[b][h][:], in0=self_term[b][h][:], in1=gain, op=ALU.mult)
-                else:
-                    nc.vector.tensor_tensor(out=self_term[b][h][:], in0=h0_acc[b, h][:], in1=gain, op=ALU.mult)
+                nc.vector.tensor_tensor(out=self_term[b][h][:], in0=h0_acc[b, h][:], in1=gain, op=ALU.mult)
                 nc.gpsimd.tensor_tensor(out=self_term[b][h][:], in0=self_term[b][h][:], in1=bias_all[:],
                                         op=ALU.add)
 
-        def a_pair(t):
-            return "xt" if t < HALVES else "sp"
+        a2_acc = {}
 
-        def half_sum_rows(t):
-            acc = bank(a_pair(t), t % HALVES, [P, NODES], "a_acc%d" % t)
-            nc.tensor.matmul(out=acc[:], lhsT=ident_b[:], rhs=adj_sb[:, t, :], start=True, stop=False)
-            nc.tensor.matmul(out=acc[:], lhsT=ident_b[:], rhs=adj2_sb[:, t, :], start=False, stop=True)
-            nc.scalar.activation(out=a_half[:, t, :].rearrange("p (s c) -> p s c", s=T),
-                                 in_=acc[:].rearrange("p (c s) -> p s c", s=T), func=ACT.Copy, scale=0.5)
-            block = a_half[:, t, t * P:(t + 1) * P]
-            nc.gpsimd.tensor_tensor(out=block, in0=block, in1=off_diag[:], op=ALU.mult)
+        def open_sum(s):
+            a2_acc[s] = bank(("sp", "xt")[s // 2], s % 2, [P, T, P], "a2_acc%d" % s)
+            for m, matrix in enumerate((adj_sb, adj2_sb)):
+                nc.tensor.matmul(out=a2_acc[s][:], lhsT=ident_b[:], start=m == 0, stop=False,
+                                 rhs=matrix.rearrange("p t (c s) -> p t s c", s=T)[:, :, s, :])
 
-        def symmetrise():
-            grouped = a_grouped[:].rearrange("p (i t) -> p i t", t=T)
-            flipped = {}
-            for s in range(T):
-                flipped[s] = bank(a_pair(s), s % HALVES, [P, T, P], "a_flipped%d" % s)
-                for t in range(T):
-                    nc.tensor.transpose(flipped[s][:, t, :], a_half[:, s, t * P:(t + 1) * P], ident_f[:])
-            for s in range(T):
-                nc.vector.tensor_tensor(out=grouped[:, s * P:(s + 1) * P, :],
-                                        in0=flipped[s][:].rearrange("p t c -> p c t"),
-                                        in1=a_half[:, :, s * P:(s + 1) * P].rearrange("p t c -> p c t"), op=ALU.add)
+        def rows_in_float32(s):
+            if s in ROWS_ADDED_BY_GPSIMD:
+                nc.gpsimd.tensor_tensor(out=rows_f[s][0][:].rearrange("p (s c) -> p s c", s=T),
+                                        in0=sorted_columns(adj_sb, s), in1=sorted_columns(adj2_sb, s), op=ALU.add)
+            else:
+                for m, matrix in enumerate((adj_sb, adj2_sb)):
+                    nc.scalar.copy(out=rows_f[s][m][:].rearrange("p (s c) -> p s c", s=T), in_=sorted_columns(matrix, s))
+
+        def close_sum(s):
+            minus = [(s, minus_diag[s][:])]
+            blocks = [(t, rows[:, t * P:(t + 1) * P]) for rows in rows_f[s] for t in range(T)]
+            addends = minus + blocks + minus
+            for i, (t, block) in enumerate(addends):
+                nc.tensor.matmul(out=a2_acc[s][:, t, :], lhsT=block, rhs=ident_f[:], is_transpose=True,
+                                 start=False, stop=i == len(addends) - 1)
+            nc.scalar.activation(out=a_grouped[:, s * P * PACK:(s + 1) * P * PACK].rearrange("p (c t) -> p c t", t=T),
+                                 in_=a2_acc[s][:].rearrange("p t c -> p c t"), func=ACT.Copy, scale=0.5)
 
         def aggregate(b):
-            rows = out[b].rearrange("(p t) c -> p t c", t=T)
             acc = {}
             for h in range(HALVES):
-                acc[h] = bank(("xt", "sp", "h1", "h0")[b], h, [P, T_HALF, COUT], "agg_acc%d_%d" % (b, h))
+                acc[h] = bank(("sp", "xt", "h1", "h0")[b], h, [P, T_HALF, COUT], "agg_acc%d_%d" % (b, h))
                 for tt in range(T_HALF):
                     s = h * T_HALF + tt
                     mx(acc[h][:, tt, :], a_codes[:, s * P:(s + 1) * P], a_scales[:, s * P:(s + 1) * P],
                        g_codes[:, b * COUT:(b + 1) * COUT], g_scales[:, b * COUT:(b + 1) * COUT])
+            agg_acc[b] = acc
+
+        def finish(b):
+            rows = out[b].rearrange("(p t) c -> p t c", t=T)
             for h in range(HALVES):
-                nc.vector.tensor_tensor(out=result[b][h][:], in0=acc[h][:], in1=self_term[b][h][:], op=ALU.add)
+                nc.vector.tensor_tensor(out=result[b][h][:], in0=agg_acc[b][h][:], in1=self_term[b][h][:], op=ALU.add)
                 nc.sync.dma_start(out=rows[:, h * T_HALF:(h + 1) * T_HALF, :], in_=result[b][h][:])
+
+        def modulate(b):
+            for h in range(HALVES):
+                modulate_h1(b, h)
 
         transpose_x(0)
         regroup_w(1, nc.vector.tensor_copy)
-        regroup_w(0, nc.scalar.copy)
         quantise(w_codes[1][:], w_scales[1][:], w_grouped[1][:])
         quantise(x_codes[0][:], x_scales[0][:], x_grouped[0][:])
         transpose_x(1)
         spread_bias()
+        project_h1(0)
+        modulate(0)
+        quantise(x_codes[1][:], x_scales[1][:], x_grouped[1][:])
+        transpose_x(2)
+        project_h1(1)
+        regroup_w(0, nc.vector.tensor_copy)
+        modulate(1)
+        mask_diagonals()
+        quantise(x_codes[2][:], x_scales[2][:], x_grouped[2][:])
+        quantise(w_codes[0][:], w_scales[0][:], w_grouped[0][:])
+        open_sum(0)
+        rows_in_float32(2)
+        rows_in_float32(0)
+        transpose_x(3)
+        project_h1(2)
+        gather_diagonal()
+        open_sum(1)
+        project_h0(0)
+        rows_in_float32(3)
         self_gain()
-        for b in range(B):
-            project_h1(b)
-            if b == 1:
-                transpose_x(3)
-            modulate_h1(b, 0)
-            if b == 0:
-                quantise(w_codes[0][:], w_scales[0][:], w_grouped[0][:])
-            modulate_h1(b, 1)
-            project_h0(b)
-            if b == 0:
-                transpose_x(2)
-            if b == 2:
-                for t in range(T):
-                    half_sum_rows(t)
-            if b < B - 1:
-                quantise(x_codes[b + 1][:], x_scales[b + 1][:], x_grouped[b + 1][:])
-            if b >= 2:
-                quantise_g(b - 2)
-            if b == B - 1:
-                symmetrise()
-                quantise(a_codes[:], a_scales[:], a_grouped[:])
-            add_self_term(b)
-        for b in range(B):
-            aggregate(b)
+        negative_diagonals()
+        quantise_g(0)
+        modulate(2)
+        quantise(x_codes[3][:], x_scales[3][:], x_grouped[3][:])
+        open_sum(2)
+        rows_in_float32(1)
+        add_self_term(0)
+        project_h1(3)
+        close_sum(0)
+        project_h0(1)
+        modulate(3)
+        close_sum(1)
+        close_sum(2)
+        open_sum(3)
+        add_self_term(1)
+        project_h0(2)
+        close_sum(3)
+        quantise_g(1)
+        add_self_term(2)
+        project_h0(3)
+        quantise(a_codes[:], a_scales[:], a_grouped[:])
+        add_self_term(3)
+        aggregate(0)
+        aggregate(1)
+        finish(0)
+        aggregate(2)
+        aggregate(3)
+        for b in range(1, B):
+            finish(b)

@@ -23,7 +23,7 @@ T = NODES // P
 HALVES = 2
 T_HALF = T // HALVES
 RUN = 4
-ROWS_ADDED_BY_GPSIMD = (2, 3)
+BIAS_BY_SCALAR = 2
 
 
 def tile_modulatedgraphconv_pa_kernel(tc, x, W, M, adj, adj2, bias, out):
@@ -112,8 +112,9 @@ def tile_modulatedgraphconv_pa_kernel(tc, x, W, M, adj, adj2, bias, out):
         minus_diag = [keep.tile([P, P], F32, name="minus_diag%d" % s) for s in range(T)]
         a_self_m = keep.tile([P, T, COUT], F32, name="a_self_m")
         diagonals = [keep.tile([P, T, P], BF16, name="diagonals%d" % m) for m in range(2)]
-        rows_f = [[keep.tile([P, NODES], F32, name="rows_f%d_%d" % (s, m))
-                   for m in range(1 if s in ROWS_ADDED_BY_GPSIMD else 2)] for s in range(T)]
+        rows_f = [keep.tile([P, NODES], F32, name="rows_f%d" % s) for s in range(T)]
+        bias_col = keep.tile([P, HALVES], F32, name="bias_col")
+        agg_t = [keep.tile([P, NODES], F32, name="agg_t%d" % h) for h in range(HALVES)]
         self_term = [[keep.tile([P, T_HALF, COUT], F32, name="self_term%d_%d" % (b, h)) for h in range(HALVES)]
                      for b in range(B)]
         result = [[keep.tile([P, T_HALF, COUT], F32, name="result%d_%d" % (b, h)) for h in range(HALVES)]
@@ -135,10 +136,15 @@ def tile_modulatedgraphconv_pa_kernel(tc, x, W, M, adj, adj2, bias, out):
                  in_=w_sb[w][:].rearrange("q u (e c i) -> q c (u e) i", e=2, i=RUN))
 
         def spread_bias():
-            acc = bank("sp", 0, [P, COUT], "bias_acc")
+            acc = bank("h0", 0, [P, COUT], "bias_acc")
             nc.tensor.matmul(out=acc[:], lhsT=ones_b[:], rhs=bias_row[:], start=True, stop=True)
             for r in range(T_HALF):
                 nc.scalar.copy(out=bias_all[:, r, :], in_=acc[:])
+            col = bank("h0", 1, [P, HALVES], "bias_col_acc")
+            for h in range(HALVES):
+                nc.tensor.matmul(out=col[:, h:h + 1], lhsT=bias_row[:, h * P:(h + 1) * P], rhs=ones_b[:, 0:1],
+                                 start=True, stop=True)
+            nc.scalar.copy(out=bias_col[:], in_=col[:])
 
         def sorted_columns(matrix, t):
             return matrix[:, t, :].rearrange("p (c s) -> p s c", s=T)
@@ -159,11 +165,14 @@ def tile_modulatedgraphconv_pa_kernel(tc, x, W, M, adj, adj2, bias, out):
         def self_gain():
             for t in range(T):
                 nc.scalar.activation(out=a_self_m[:, t, :], in_=m_sb[:, t, :], func=ACT.Copy, scale=a_self[:, t:t + 1])
-
-        def negative_diagonals():
-            nc.scalar.activation(out=a_self_neg[:], in_=a_self[:], func=ACT.Copy, scale=-1.0)
+            nc.scalar.activation(out=a_self_neg[:], in_=a_self[:], func=ACT.Copy, scale=-2.0)
             for s in range(T):
                 nc.scalar.activation(out=minus_diag[s][:], in_=ident_f[:], func=ACT.Copy, scale=a_self_neg[:, s:s + 1])
+
+        def warm_up():
+            acc = bank("h0", 0, [P, P], "warm_acc")
+            for i in range(2):
+                nc.tensor.matmul(out=acc[:], lhsT=ident_f[:], rhs=ident_f[:], start=True, stop=True)
 
         h1_acc = {}
         agg_acc = {}
@@ -203,8 +212,9 @@ def tile_modulatedgraphconv_pa_kernel(tc, x, W, M, adj, adj2, bias, out):
             for h in range(HALVES):
                 gain = a_self_m[:, h * T_HALF:(h + 1) * T_HALF, :]
                 nc.vector.tensor_tensor(out=self_term[b][h][:], in0=h0_acc[b, h][:], in1=gain, op=ALU.mult)
-                nc.gpsimd.tensor_tensor(out=self_term[b][h][:], in0=self_term[b][h][:], in1=bias_all[:],
-                                        op=ALU.add)
+                if b != BIAS_BY_SCALAR:
+                    nc.gpsimd.tensor_tensor(out=self_term[b][h][:], in0=self_term[b][h][:], in1=bias_all[:],
+                                            op=ALU.add)
 
         a2_acc = {}
 
@@ -214,18 +224,12 @@ def tile_modulatedgraphconv_pa_kernel(tc, x, W, M, adj, adj2, bias, out):
                 nc.tensor.matmul(out=a2_acc[s][:], lhsT=ident_b[:], start=m == 0, stop=False,
                                  rhs=matrix.rearrange("p t (c s) -> p t s c", s=T)[:, :, s, :])
 
-        def rows_in_float32(s):
-            if s in ROWS_ADDED_BY_GPSIMD:
-                nc.gpsimd.tensor_tensor(out=rows_f[s][0][:].rearrange("p (s c) -> p s c", s=T),
-                                        in0=sorted_columns(adj_sb, s), in1=sorted_columns(adj2_sb, s), op=ALU.add)
-            else:
-                for m, matrix in enumerate((adj_sb, adj2_sb)):
-                    nc.scalar.copy(out=rows_f[s][m][:].rearrange("p (s c) -> p s c", s=T), in_=sorted_columns(matrix, s))
+        def add_rows(s):
+            nc.gpsimd.tensor_tensor(out=rows_f[s][:].rearrange("p (s c) -> p s c", s=T),
+                                    in0=sorted_columns(adj_sb, s), in1=sorted_columns(adj2_sb, s), op=ALU.add)
 
         def close_sum(s):
-            minus = [(s, minus_diag[s][:])]
-            blocks = [(t, rows[:, t * P:(t + 1) * P]) for rows in rows_f[s] for t in range(T)]
-            addends = minus + blocks + minus
+            addends = [(t, rows_f[s][:, t * P:(t + 1) * P]) for t in range(T)] + [(s, minus_diag[s][:])]
             for i, (t, block) in enumerate(addends):
                 nc.tensor.matmul(out=a2_acc[s][:, t, :], lhsT=block, rhs=ident_f[:], is_transpose=True,
                                  start=False, stop=i == len(addends) - 1)
@@ -242,6 +246,23 @@ def tile_modulatedgraphconv_pa_kernel(tc, x, W, M, adj, adj2, bias, out):
                        g_codes[:, b * COUT:(b + 1) * COUT], g_scales[:, b * COUT:(b + 1) * COUT])
             agg_acc[b] = acc
 
+        def aggregate_by_channels(b):
+            for h in range(HALVES):
+                acc = bank("h1", h, [P, NODES], "agg_t_acc%d" % h)
+                first = b * COUT + h * P
+                mx(acc[:], g_codes[:, first:first + P], g_scales[:, first:first + P], a_codes[:], a_scales[:])
+                nc.scalar.activation(out=agg_t[h][:], in_=acc[:], func=ACT.Identity, bias=bias_col[:, h:h + 1])
+
+        def turn_aggregate(b):
+            agg_acc[b] = {}
+            for h in range(HALVES):
+                agg_acc[b][h] = bank("h1", h, [P, T_HALF, COUT], "agg_acc%d_%d" % (b, h))
+                for tt in range(T_HALF):
+                    s = h * T_HALF + tt
+                    for ch in range(HALVES):
+                        nc.tensor.transpose(agg_acc[b][h][:, tt, ch * P:(ch + 1) * P],
+                                            agg_t[ch][:, s * P:(s + 1) * P], ident_f[:])
+
         def finish(b):
             rows = out[b].rearrange("(p t) c -> p t c", t=T)
             for h in range(HALVES):
@@ -252,58 +273,58 @@ def tile_modulatedgraphconv_pa_kernel(tc, x, W, M, adj, adj2, bias, out):
             for h in range(HALVES):
                 modulate_h1(b, h)
 
+        warm_up()
         transpose_x(0)
         regroup_w(1, nc.vector.tensor_copy)
         quantise(w_codes[1][:], w_scales[1][:], w_grouped[1][:])
         quantise(x_codes[0][:], x_scales[0][:], x_grouped[0][:])
         transpose_x(1)
-        spread_bias()
         project_h1(0)
+        regroup_w(0, nc.scalar.copy)
         modulate(0)
         quantise(x_codes[1][:], x_scales[1][:], x_grouped[1][:])
         transpose_x(2)
         project_h1(1)
-        regroup_w(0, nc.vector.tensor_copy)
+        spread_bias()
+        quantise(w_codes[0][:], w_scales[0][:], w_grouped[0][:])
         modulate(1)
         mask_diagonals()
         quantise(x_codes[2][:], x_scales[2][:], x_grouped[2][:])
-        quantise(w_codes[0][:], w_scales[0][:], w_grouped[0][:])
         open_sum(0)
-        rows_in_float32(2)
-        rows_in_float32(0)
+        open_sum(1)
+        add_rows(0)
+        add_rows(1)
         transpose_x(3)
         project_h1(2)
         gather_diagonal()
-        open_sum(1)
+        open_sum(2)
         project_h0(0)
-        rows_in_float32(3)
+        add_rows(2)
+        add_rows(3)
         self_gain()
-        negative_diagonals()
         quantise_g(0)
         modulate(2)
         quantise(x_codes[3][:], x_scales[3][:], x_grouped[3][:])
-        open_sum(2)
-        rows_in_float32(1)
+        open_sum(3)
         add_self_term(0)
         project_h1(3)
         close_sum(0)
         project_h0(1)
         modulate(3)
         close_sum(1)
-        close_sum(2)
-        open_sum(3)
         add_self_term(1)
-        project_h0(2)
+        close_sum(2)
         close_sum(3)
+        project_h0(2)
         quantise_g(1)
         add_self_term(2)
         project_h0(3)
         quantise(a_codes[:], a_scales[:], a_grouped[:])
         add_self_term(3)
+        aggregate_by_channels(2)
         aggregate(0)
         aggregate(1)
-        finish(0)
-        aggregate(2)
+        turn_aggregate(2)
         aggregate(3)
-        for b in range(1, B):
+        for b in range(B):
             finish(b)

from contextlib import ExitStack

import concourse.mybir as mybir
from concourse.masks import make_identity

FLOPS = 2 * 2048 * 512 * 512 + 4 * 2 * 512 * 512 * 256

F32 = mybir.dt.float32
BF16 = mybir.dt.bfloat16
U32 = mybir.dt.uint32
U8 = mybir.dt.uint8
FP8X4 = mybir.dt.float8_e4m3fn_x4
ALU = mybir.AluOpType
ACT = mybir.ActivationFunctionType

P = 128
PACK = 4
B = 4
NODES = 512
CIN = 512
COUT = 256
T = NODES // P
HALVES = 2
T_HALF = T // HALVES
RUN = 4
BIAS_BY_SCALAR = 2


def tile_modulatedgraphconv_pa_kernel(tc, x, W, M, adj, adj2, bias, out):
    nc = tc.nc
    with ExitStack() as ctx:
        const = ctx.enter_context(tc.tile_pool(name="const", bufs=1))
        keep = ctx.enter_context(tc.tile_pool(name="keep", bufs=1))
        psum = ctx.enter_context(tc.psum_pool(name="psum", bufs=1))
        ctx.enter_context(tc.manual_schedule())

        def bank(pair, i, shape, name):
            return psum.tile(shape, F32, tag="%s%d" % (pair, i), name=name)

        ident_f = const.tile([P, P], F32, name="ident_f")
        ident_b = const.tile([P, P], BF16, name="ident_b")
        ident_4 = const.tile([P, T, P], BF16, name="ident_4")
        ones_b = const.tile([P, P], BF16, name="ones_b")
        bias_row = const.tile([P, COUT], BF16, name="bias_row")
        warm_in = const.tile([P, 1], F32, name="warm_in")
        warm_out = const.tile([P, 1], F32, name="warm_out")

        nc.gpsimd.memset(bias_row[:], 0.0)
        make_identity(nc, ident_f[:])
        nc.gpsimd.memset(warm_in[:], 0.0)
        nc.gpsimd.memset(ones_b[:], 1.0)
        make_identity(nc, ident_b[:])

        x_sb = [keep.tile([P, T * CIN], BF16, name="x_sb%d" % b) for b in range(B)]
        w_sb = [keep.tile([P, 2, 2 * COUT], BF16, name="w_sb%d" % w) for w in range(2)]
        m_sb = keep.tile([P, T, COUT], BF16, name="m_sb")
        adj_flat = [keep.tile([P, T * (NODES + 1)], BF16, name="adj_flat%d" % m) for m in range(2)]
        adj_sb, adj2_sb = [flat[:, 0:T * NODES].rearrange("p (t i) -> p t i", t=T) for flat in adj_flat]

        nc.scalar.dma_start(out=bias_row[0:1, :], in_=bias.rearrange("(o c) -> o c", o=1))
        nc.scalar.activation(out=warm_out[:], in_=warm_in[:], func=ACT.Copy)
        for t in range(T):
            nc.scalar.copy(out=ident_4[:, t, :], in_=ident_b[:])

        for h in range(HALVES):
            nc.sync.dma_start(
                out=x_sb[0][:, h * T_HALF * CIN:(h + 1) * T_HALF * CIN].rearrange("p (t k) -> p t k", t=T_HALF),
                in_=x[0].rearrange("(p t) k -> p t k", t=T)[:, h * T_HALF:(h + 1) * T_HALF, :])
        def load_w(w):
            nc.sync.dma_start(out=w_sb[w][:], in_=W[w].rearrange("(u q e) c -> q u (e c)", u=2, q=P, e=2))

        load_w(1)
        nc.sync.dma_start(out=x_sb[1][:], in_=x[1].rearrange("(p t) k -> p (t k)", t=T))
        nc.sync.dma_start(out=m_sb[:], in_=M.rearrange("(p t) c -> p t c", t=T))
        load_w(0)
        nc.sync.dma_start(out=x_sb[2][:], in_=x[2].rearrange("(p t) k -> p (t k)", t=T))
        nc.sync.dma_start(out=adj_sb, in_=adj.rearrange("(p t) i -> p t i", t=T))
        nc.sync.dma_start(out=adj2_sb, in_=adj2.rearrange("(p t) i -> p t i", t=T))
        nc.sync.dma_start(out=x_sb[3][:], in_=x[3].rearrange("(p t) k -> p (t k)", t=T))

        XW = T * P
        w_grouped = [keep.tile([P, COUT * PACK], BF16, name="w_grouped%d" % w, align_bytes=64) for w in range(2)]
        w_codes = [keep.tile([P, COUT], U32, name="w_codes%d" % w, align_bytes=64) for w in range(2)]
        w_scales = [keep.tile([P, COUT], U8, name="w_scales%d" % w, align_bytes=64) for w in range(2)]
        x_batches = ((0,), (1,), (2,), (3,))
        x_grouped = [keep.tile([P, len(bs) * XW * PACK], BF16, name="x_grouped%d" % i, align_bytes=64)
                     for i, bs in enumerate(x_batches)]
        x_codes = [keep.tile([P, len(bs) * XW], U32, name="x_codes%d" % i, align_bytes=64)
                   for i, bs in enumerate(x_batches)]
        x_scales = [keep.tile([P, len(bs) * XW], U8, name="x_scales%d" % i, align_bytes=64)
                    for i, bs in enumerate(x_batches)]
        g_grouped = keep.tile([P, B * COUT * PACK], BF16, name="g_grouped", align_bytes=64)
        g_codes = keep.tile([P, B * COUT], U32, name="g_codes", align_bytes=64)
        g_scales = keep.tile([P, B * COUT], U8, name="g_scales", align_bytes=64)
        a_grouped = keep.tile([P, NODES * PACK], BF16, name="a_grouped", align_bytes=64)
        a_codes = keep.tile([P, NODES], U32, name="a_codes", align_bytes=64)
        a_scales = keep.tile([P, NODES], U8, name="a_scales", align_bytes=64)

        def x_part(tiles, b, width):
            return tiles[b][:, 0:width]

        def quantise(codes, scales, grouped):
            nc.vector.quantize_mx(out=codes.bitcast(FP8X4), scales=scales, in_=grouped)

        def mx(acc, lhs_codes, lhs_scales, rhs_codes, rhs_scales):
            nc.tensor.matmul_mx(out=acc, lhsT=lhs_codes.bitcast(FP8X4), lhsT_scale=lhs_scales,
                                rhs=rhs_codes.bitcast(FP8X4), rhs_scale=rhs_scales, start=True, stop=True)

        bias_all = keep.tile([P, T_HALF, COUT], F32, name="bias_all")
        a_self = keep.tile([P, T], F32, name="a_self")
        a_self_neg = keep.tile([P, T], F32, name="a_self_neg")
        minus_diag = [keep.tile([P, P], F32, name="minus_diag%d" % s) for s in range(T)]
        a_self_m = keep.tile([P, T, COUT], F32, name="a_self_m")
        diagonals = [keep.tile([P, T, P], BF16, name="diagonals%d" % m) for m in range(2)]
        rows_f = [keep.tile([P, NODES], F32, name="rows_f%d" % s) for s in range(T)]
        bias_col = keep.tile([P, HALVES], F32, name="bias_col")
        agg_t = [keep.tile([P, NODES], F32, name="agg_t%d" % h) for h in range(HALVES)]
        self_term = [[keep.tile([P, T_HALF, COUT], F32, name="self_term%d_%d" % (b, h)) for h in range(HALVES)]
                     for b in range(B)]
        result = [[keep.tile([P, T_HALF, COUT], F32, name="result%d_%d" % (b, h)) for h in range(HALVES)]
                  for b in range(B)]

        def transpose_x(b):
            words = x_sb[b][:].bitcast(F32).rearrange("p (t u q) -> p t u q", t=T, u=2)
            grouped = x_part(x_grouped, b, XW * PACK).bitcast(F32).rearrange("q (t n u) -> q t n u", t=T, u=2)
            for h in range(HALVES):
                x_t = bank("xt", h, [P, T_HALF, 2, P], "x_t%d_%d" % (b, h))
                for tt in range(T_HALF):
                    for u in range(2):
                        nc.tensor.transpose(x_t[:, tt, u, :], words[:, h * T_HALF + tt, u, :], ident_f[:])
                nc.scalar.copy(out=grouped[:, h * T_HALF:(h + 1) * T_HALF, :, :],
                               in_=x_t[:].rearrange("q t u n -> q t n u"))

        def regroup_w(w, copy):
            copy(out=w_grouped[w][:].rearrange("q (c i s) -> q c s i", i=RUN, s=PACK),
                 in_=w_sb[w][:].rearrange("q u (e c i) -> q c (u e) i", e=2, i=RUN))

        def spread_bias():
            acc = bank("h0", 0, [P, COUT], "bias_acc")
            nc.tensor.matmul(out=acc[:], lhsT=ones_b[:], rhs=bias_row[:], start=True, stop=True)
            for r in range(T_HALF):
                nc.scalar.copy(out=bias_all[:, r, :], in_=acc[:])
            col = bank("h0", 1, [P, HALVES], "bias_col_acc")
            for h in range(HALVES):
                nc.tensor.matmul(out=col[:, h:h + 1], lhsT=bias_row[:, h * P:(h + 1) * P], rhs=ones_b[:, 0:1],
                                 start=True, stop=True)
            nc.scalar.copy(out=bias_col[:], in_=col[:])

        def sorted_columns(matrix, t):
            return matrix[:, t, :].rearrange("p (c s) -> p s c", s=T)

        def mask_diagonals():
            for m in range(2):
                blocks = adj_flat[m][:].rearrange("p (t r) -> p t r", t=T)[:, :, 0:NODES:T]
                nc.gpsimd.tensor_tensor(out=diagonals[m][:], in0=blocks, in1=ident_4[:], op=ALU.mult)

        def gather_diagonal():
            acc = bank("h0", 0, [P, T], "diag_acc")
            for t in range(T):
                for m in range(2):
                    nc.tensor.matmul(out=acc[:, t:t + 1], lhsT=diagonals[m][:, t, :], rhs=ones_b[:, 0:1],
                                     start=m == 0, stop=m == 1)
            nc.scalar.copy(out=a_self[:], in_=acc[:])

        def self_gain():
            for t in range(T):
                nc.scalar.activation(out=a_self_m[:, t, :], in_=m_sb[:, t, :], func=ACT.Copy, scale=a_self[:, t:t + 1])
            nc.scalar.activation(out=a_self_neg[:], in_=a_self[:], func=ACT.Copy, scale=-2.0)
            for s in range(T):
                nc.scalar.activation(out=minus_diag[s][:], in_=ident_f[:], func=ACT.Copy, scale=a_self_neg[:, s:s + 1])

        def warm_up():
            acc = bank("h0", 0, [P, P], "warm_acc")
            for i in range(2):
                nc.tensor.matmul(out=acc[:], lhsT=ident_f[:], rhs=ident_f[:], start=True, stop=True)

        h1_acc = {}
        agg_acc = {}
        h0_acc = {}

        def project_h1(b):
            codes = x_part(x_codes, b, XW)
            scales = x_part(x_scales, b, XW)
            for h in range(HALVES):
                h1_acc[b, h] = bank("h1", h, [P, T, P], "h1_acc%d_%d" % (b, h))
                for t in range(T):
                    mx(h1_acc[b, h][:, t, :], codes[:, t * P:(t + 1) * P], scales[:, t * P:(t + 1) * P],
                       w_codes[1][:, h * P:(h + 1) * P], w_scales[1][:, h * P:(h + 1) * P])

        def project_h0(b):
            codes = x_part(x_codes, b, XW)
            scales = x_part(x_scales, b, XW)
            for h in range(HALVES):
                h0_acc[b, h] = bank("h0", h, [P, T_HALF, COUT], "h0_acc%d_%d" % (b, h))
                for tt in range(T_HALF):
                    t = h * T_HALF + tt
                    mx(h0_acc[b, h][:, tt, :], codes[:, t * P:(t + 1) * P], scales[:, t * P:(t + 1) * P],
                       w_codes[0][:], w_scales[0][:])

        def modulate_h1(b, h):
            grouped = g_grouped[:, b * COUT * PACK:(b + 1) * COUT * PACK].rearrange("p (c t) -> p c t", t=T)
            nc.vector.tensor_tensor(out=grouped[:, h * P:(h + 1) * P, :],
                                    in0=h1_acc[b, h][:].rearrange("p t c -> p c t"),
                                    in1=m_sb[:, :, h * P:(h + 1) * P].rearrange("p t c -> p c t"), op=ALU.mult)

        def quantise_g(i):
            w = 2 * COUT
            quantise(g_codes[:, i * w:(i + 1) * w], g_scales[:, i * w:(i + 1) * w],
                     g_grouped[:, i * w * PACK:(i + 1) * w * PACK])

        def add_self_term(b):
            for h in range(HALVES):
                gain = a_self_m[:, h * T_HALF:(h + 1) * T_HALF, :]
                nc.vector.tensor_tensor(out=self_term[b][h][:], in0=h0_acc[b, h][:], in1=gain, op=ALU.mult)
                if b != BIAS_BY_SCALAR:
                    nc.gpsimd.tensor_tensor(out=self_term[b][h][:], in0=self_term[b][h][:], in1=bias_all[:],
                                            op=ALU.add)

        a2_acc = {}

        def open_sum(s):
            a2_acc[s] = bank(("sp", "xt")[s // 2], s % 2, [P, T, P], "a2_acc%d" % s)
            for m, matrix in enumerate((adj_sb, adj2_sb)):
                nc.tensor.matmul(out=a2_acc[s][:], lhsT=ident_b[:], start=m == 0, stop=False,
                                 rhs=matrix.rearrange("p t (c s) -> p t s c", s=T)[:, :, s, :])

        def add_rows(s):
            nc.gpsimd.tensor_tensor(out=rows_f[s][:].rearrange("p (s c) -> p s c", s=T),
                                    in0=sorted_columns(adj_sb, s), in1=sorted_columns(adj2_sb, s), op=ALU.add)

        def close_sum(s):
            addends = [(t, rows_f[s][:, t * P:(t + 1) * P]) for t in range(T)] + [(s, minus_diag[s][:])]
            for i, (t, block) in enumerate(addends):
                nc.tensor.matmul(out=a2_acc[s][:, t, :], lhsT=block, rhs=ident_f[:], is_transpose=True,
                                 start=False, stop=i == len(addends) - 1)
            nc.scalar.activation(out=a_grouped[:, s * P * PACK:(s + 1) * P * PACK].rearrange("p (c t) -> p c t", t=T),
                                 in_=a2_acc[s][:].rearrange("p t c -> p c t"), func=ACT.Copy, scale=0.5)

        def aggregate(b):
            acc = {}
            for h in range(HALVES):
                acc[h] = bank(("sp", "xt", "h1", "h0")[b], h, [P, T_HALF, COUT], "agg_acc%d_%d" % (b, h))
                for tt in range(T_HALF):
                    s = h * T_HALF + tt
                    mx(acc[h][:, tt, :], a_codes[:, s * P:(s + 1) * P], a_scales[:, s * P:(s + 1) * P],
                       g_codes[:, b * COUT:(b + 1) * COUT], g_scales[:, b * COUT:(b + 1) * COUT])
            agg_acc[b] = acc

        def aggregate_by_channels(b):
            for h in range(HALVES):
                acc = bank("h1", h, [P, NODES], "agg_t_acc%d" % h)
                first = b * COUT + h * P
                mx(acc[:], g_codes[:, first:first + P], g_scales[:, first:first + P], a_codes[:], a_scales[:])
                nc.scalar.activation(out=agg_t[h][:], in_=acc[:], func=ACT.Identity, bias=bias_col[:, h:h + 1])

        def turn_aggregate(b):
            agg_acc[b] = {}
            for h in range(HALVES):
                agg_acc[b][h] = bank("h1", h, [P, T_HALF, COUT], "agg_acc%d_%d" % (b, h))
                for tt in range(T_HALF):
                    s = h * T_HALF + tt
                    for ch in range(HALVES):
                        nc.tensor.transpose(agg_acc[b][h][:, tt, ch * P:(ch + 1) * P],
                                            agg_t[ch][:, s * P:(s + 1) * P], ident_f[:])

        def finish(b):
            rows = out[b].rearrange("(p t) c -> p t c", t=T)
            for h in range(HALVES):
                nc.vector.tensor_tensor(out=result[b][h][:], in0=agg_acc[b][h][:], in1=self_term[b][h][:], op=ALU.add)
                nc.sync.dma_start(out=rows[:, h * T_HALF:(h + 1) * T_HALF, :], in_=result[b][h][:])

        def modulate(b):
            for h in range(HALVES):
                modulate_h1(b, h)

        warm_up()
        transpose_x(0)
        regroup_w(1, nc.vector.tensor_copy)
        quantise(w_codes[1][:], w_scales[1][:], w_grouped[1][:])
        quantise(x_codes[0][:], x_scales[0][:], x_grouped[0][:])
        transpose_x(1)
        project_h1(0)
        regroup_w(0, nc.scalar.copy)
        modulate(0)
        quantise(x_codes[1][:], x_scales[1][:], x_grouped[1][:])
        transpose_x(2)
        project_h1(1)
        spread_bias()
        quantise(w_codes[0][:], w_scales[0][:], w_grouped[0][:])
        modulate(1)
        mask_diagonals()
        quantise(x_codes[2][:], x_scales[2][:], x_grouped[2][:])
        open_sum(0)
        open_sum(1)
        add_rows(0)
        add_rows(1)
        transpose_x(3)
        project_h1(2)
        gather_diagonal()
        open_sum(2)
        project_h0(0)
        add_rows(2)
        add_rows(3)
        self_gain()
        quantise_g(0)
        modulate(2)
        quantise(x_codes[3][:], x_scales[3][:], x_grouped[3][:])
        open_sum(3)
        add_self_term(0)
        project_h1(3)
        close_sum(0)
        project_h0(1)
        modulate(3)
        close_sum(1)
        add_self_term(1)
        close_sum(2)
        close_sum(3)
        project_h0(2)
        quantise_g(1)
        add_self_term(2)
        project_h0(3)
        quantise(a_codes[:], a_scales[:], a_grouped[:])
        add_self_term(3)
        aggregate_by_channels(2)
        aggregate(0)
        aggregate(1)
        turn_aggregate(2)
        aggregate(3)
        for b in range(B):
            finish(b)
